import numpy as np
import ml_dtypes


def mxq(x, axis, fmt="e4m3"):
    dtype, down = {"e4m3": (ml_dtypes.float8_e4m3fn, 7), "e5m2": (ml_dtypes.float8_e5m2, 14)}[fmt]
    v = np.moveaxis(np.asarray(x, np.float32).astype(ml_dtypes.bfloat16).astype(np.float64), axis, -1)
    blocks = v.reshape(v.shape[:-1] + (-1, 32))
    amax = np.abs(blocks).max(-1, keepdims=True)
    byte = np.maximum(np.where(amax > 0, np.frexp(amax)[1] - 1 + 127, 0) - down, 1)
    scale = np.exp2(byte - 127.0)
    codes = (blocks / scale).astype(np.float32).astype(dtype).astype(np.float64)
    return np.moveaxis((codes * scale).reshape(v.shape), -1, axis)


WIDE = False


def mx_kscale(k):
    if not WIDE:
        return np.ones(k)
    levels = np.array([10, -10, 5, -5, 0])
    if k % 512:
        return np.exp2(np.random.permutation(np.resize(levels, k // 32))).repeat(32)
    a = np.empty((k // 512, 16))
    for p in range(k // 512):
        a[p, :8] = np.random.permutation(np.resize(levels, 8))
        for g in range(8):
            far = levels[np.abs(levels - a[p, g]) >= 10]
            a[p, g + 8] = far[np.random.randint(len(far))]
    return np.exp2(a.ravel()).repeat(32)


BF16 = ml_dtypes.bfloat16


def bf(x):
    return np.asarray(x, np.float32).astype(BF16)


def f64(x):
    return np.asarray(x).astype(np.float64)


N, IN_F, J, K = 256, 2048, 128, 16


def setup_inputs():
    s = mx_kscale(IN_F)
    s = s / s.max()
    return {"tensor": bf(np.random.standard_normal((N, IN_F)) * s),
            "T": bf(np.random.standard_normal((IN_F, J, K)) * 4.0 / (K * np.sqrt(IN_F)) / s[:, None, None])}


def reference(tensor, T):
    x = f64(tensor).reshape(tensor.shape[0], -1)
    feats = (mxq(x, 1, "e4m3") @ mxq(f64(T).reshape(IN_F, J * K), 0, "e4m3")).reshape(N, J, K)
    diversity = np.stack([np.exp(-np.abs(feats[n][None, :, :] - feats).sum(axis=2)).sum(axis=0) for n in range(N)])
    return np.concatenate((x, diversity), axis=1)

@@ -1,0 +1,309 @@
+from contextlib import ExitStack
+
+import concourse.mybir as mybir
+from concourse.masks import make_identity
+
+F32 = mybir.dt.float32
+BF16 = mybir.dt.bfloat16
+U32 = mybir.dt.uint32
+U8 = mybir.dt.uint8
+FP8X4 = mybir.dt.float8_e4m3fn_x4
+ALU = mybir.AluOpType
+ACT = mybir.ActivationFunctionType
+AXIS = mybir.AxisListType
+
+P = 128
+ROWS = 256
+ROW_BLOCKS = ROWS // P
+IN_F = 2048
+J = 128
+K = 16
+COLS = J * K
+PACK = 4
+K_PASS = P * PACK
+PASSES = IN_F // K_PASS
+BANK = 512
+COL_BLOCKS = COLS // BANK
+J_PER_BLOCK = BANK // K
+K_PER_BANK = BANK // ROWS
+F_BANKS = K // K_PER_BANK
+ROWS_PER_STEP = 6
+TREE_ROWS_PER_STEP = ROWS_PER_STEP // 3
+TREE_HALVES = (8, 4, 2, 1)
+
+FLOPS = 2 * ROWS * IN_F * COLS
+
+
+def tile_minibatchdiscriminator_kernel(tc, tensor, T, out):
+    nc = tc.nc
+    weights = T.rearrange("i j k -> i (j k)")
+
+    with ExitStack() as pools:
+        keep = pools.enter_context(tc.tile_pool(name="keep", bufs=1))
+        banks = pools.enter_context(tc.psum_pool(name="banks", bufs=1))
+
+        identity = keep.tile([P, P], F32)
+        make_identity(nc, identity[:])
+
+        x_rows = keep.tile([P, ROW_BLOCKS * IN_F], BF16)
+        nc.sync.dma_start(
+            out=x_rows[:].rearrange("p (b i) -> p b i", b=ROW_BLOCKS),
+            in_=tensor.rearrange("(b p) i -> p b i", p=P),
+        )
+
+        f_sbuf = keep.tile([P, K, ROWS], F32)
+        f_banks = []
+        k_sum = keep.tile([P, ROWS], F32)
+        chain_start = keep.tile([P, ROWS], F32)
+        from_later = keep.tile([P, ROWS], F32)
+        from_earlier = keep.tile([P, ROWS_PER_STEP, ROWS], F32)
+        diversity = keep.tile([P, ROWS], F32)
+        d_rows = keep.tile([P, ROW_BLOCKS, J], F32)
+
+        with tc.tile_pool(name="stage", bufs=1) as stage:
+            t_raw = []
+            for g in range(PASSES):
+                raw = stage.tile([P, PACK, COLS], BF16, name="t_raw%d" % g)
+                rows = weights[K_PASS * g : K_PASS * (g + 1), :].rearrange("(p t) c -> p t c", t=PACK)
+                for u in range(2):
+                    nc.sync.dma_start(
+                        out=raw[:, 2 * u : 2 * u + 2, :], in_=rows[:, 2 * u : 2 * u + 2, :]
+                    )
+                t_raw.append(raw)
+
+            x_words = x_rows[:].bitcast(F32)
+            words_per_row = IN_F // 2
+            x_grouped = stage.tile([P, PASSES * ROWS * PACK], BF16, align_bytes=64)
+            x_grouped_words = x_grouped[:].bitcast(F32).rearrange(
+                "p (g n u) -> p g n u", g=PASSES, u=2
+            )
+            for g in range(PASSES):
+                x_t = banks.tile([P, 2, ROWS], F32, name="x_t%d" % g, tag="bank%d" % g)
+                for u in range(2):
+                    for b in range(ROW_BLOCKS):
+                        first = words_per_row * b + 2 * P * g
+                        nc.tensor.transpose(
+                            x_t[:, u, b * P : (b + 1) * P],
+                            x_words[:, first + u : first + 2 * P : 2],
+                            identity[:],
+                        )
+                nc.vector.tensor_copy(
+                    out=x_grouped_words[:, g], in_=x_t[:].rearrange("p u n -> p n u")
+                )
+            x_codes = stage.tile([P, PASSES, ROWS], U32, align_bytes=64)
+            x_scales = stage.tile([P, PASSES, ROWS], U8, align_bytes=64)
+            nc.vector.quantize_mx(
+                out=x_codes[:].rearrange("p g n -> p (g n)").bitcast(FP8X4),
+                scales=x_scales[:].rearrange("p g n -> p (g n)"),
+                in_=x_grouped[:],
+            )
+
+            t_codes = stage.tile([P, PASSES, COLS], U32, align_bytes=64)
+            t_scales = stage.tile([P, PASSES, COLS], U8, align_bytes=64)
+            feats = [
+                [
+                    banks.tile(
+                        [P, BANK],
+                        F32,
+                        name="feats%d_%d" % (b, c),
+                        tag="bank%d" % (COL_BLOCKS * b + c),
+                    )
+                    for c in range(COL_BLOCKS)
+                ]
+                for b in range(ROW_BLOCKS)
+            ]
+
+            def regroup(g, c):
+                grouped = stage.tile(
+                    [P, BANK, PACK], BF16, name="t_grouped", bufs=4, align_bytes=64
+                )
+                copy = nc.vector.tensor_copy if c % 2 == 0 else nc.scalar.copy
+                copy(
+                    out=grouped[:].rearrange("p (c i) t -> p c t i", i=4),
+                    in_=t_raw[g][:, :, c * BANK : (c + 1) * BANK].rearrange(
+                        "p t (c i) -> p c t i", i=4
+                    ),
+                )
+                return grouped
+
+            def quantise_and_multiply(grouped, g, c):
+                cols = slice(c * BANK, (c + 1) * BANK)
+                nc.vector.quantize_mx(
+                    out=t_codes[:, g, cols].bitcast(FP8X4),
+                    scales=t_scales[:, g, cols],
+                    in_=grouped[:].rearrange("p c t -> p (c t)"),
+                )
+                for b in range(ROW_BLOCKS):
+                    rows = slice(b * P, (b + 1) * P)
+                    nc.tensor.matmul_mx(
+                        out=feats[b][c][:],
+                        lhsT=x_codes[:, g, rows].bitcast(FP8X4),
+                        lhsT_scale=x_scales[:, g, rows],
+                        rhs=t_codes[:, g, cols].bitcast(FP8X4),
+                        rhs_scale=t_scales[:, g, cols],
+                        start=(g == 0),
+                        stop=(g == PASSES - 1),
+                    )
+
+            pieces = [(g, c) for g in range(PASSES) for c in range(COL_BLOCKS)]
+            waiting = None
+            for g, c in pieces:
+                grouped = regroup(g, c)
+                if waiting is not None:
+                    quantise_and_multiply(*waiting)
+                waiting = (grouped, g, c)
+            quantise_and_multiply(*waiting)
+
+            f_rows = [stage.tile([P, K, J], F32, name="f_rows%d" % b) for b in range(ROW_BLOCKS)]
+            for b in range(ROW_BLOCKS):
+                for c in range(COL_BLOCKS):
+                    copy = nc.vector.tensor_copy if c % 2 == 0 else nc.scalar.copy
+                    copy(
+                        out=f_rows[b][:, :, c * J_PER_BLOCK : (c + 1) * J_PER_BLOCK],
+                        in_=feats[b][c][:].rearrange("p (j k) -> p k j", k=K),
+                    )
+            for q in range(F_BANKS):
+                f_bank = banks.tile([P, K_PER_BANK, ROWS], F32, name="f_bank%d" % q, tag="bank%d" % q)
+                for h in range(K_PER_BANK):
+                    for b in range(ROW_BLOCKS):
+                        nc.tensor.transpose(
+                            f_bank[:, h, b * P : (b + 1) * P],
+                            f_rows[b][:, K_PER_BANK * q + h, :],
+                            identity[:],
+                        )
+                copy = nc.vector.tensor_copy if q % 2 == 0 else nc.scalar.copy
+                copy(out=f_sbuf[:, K_PER_BANK * q : K_PER_BANK * (q + 1), :], in_=f_bank[:])
+                f_banks.append(f_bank)
+
+        work = pools.enter_context(tc.tile_pool(name="work", bufs=3))
+
+        nc.vector.tensor_reduce(
+            out=k_sum[:], in_=f_sbuf[:].rearrange("p k n -> p n k"), axis=AXIS.X, op=ALU.add
+        )
+        nc.vector.tensor_scalar_mul(out=chain_start[:], in0=k_sum[:], scalar1=-0.5)
+        nc.vector.memset(from_later[:], 0.0)
+        nc.vector.memset(from_earlier[:], 0.0)
+
+        steps = [
+            list(range(first, min(first + ROWS_PER_STEP, ROWS - 1)))
+            for first in range(0, ROWS - 1, ROWS_PER_STEP)
+        ]
+
+        def chain_rows(rows):
+            return [n for n in rows if n % 3 != 2]
+
+        def tree_rows(rows):
+            return [n for n in rows if n % 3 == 2]
+
+        def chains(rows):
+            acc = work.tile([P, ROWS_PER_STEP, ROWS], F32, name="acc")
+            for k in range(K):
+                for n in rows:
+                    later = slice(n + 1, ROWS)
+                    nc.vector.scalar_tensor_tensor(
+                        out=acc[:, n % ROWS_PER_STEP, later],
+                        in0=f_banks[k // K_PER_BANK][:, k % K_PER_BANK, later],
+                        scalar=f_sbuf[:, k, n : n + 1],
+                        in1=chain_start[:, later] if k == 0 else acc[:, n % ROWS_PER_STEP, later],
+                        op0=ALU.max,
+                        op1=ALU.add,
+                    )
+            return acc
+
+        def absolute_differences(rows):
+            leaves = work.tile([P, TREE_ROWS_PER_STEP, K, ROWS], F32, name="leaves", bufs=2)
+            later = slice(rows[0] + 1, ROWS)
+            for r, n in enumerate(rows):
+                for k in range(K):
+                    nc.scalar.activation(
+                        out=leaves[:, r, k, later],
+                        in_=f_sbuf[:, k, later],
+                        func=ACT.Abs,
+                        bias=f_sbuf[:, k, n : n + 1],
+                        scale=-1.0,
+                    )
+            return leaves
+
+        def add_tree(rows, leaves):
+            later = slice(rows[0] + 1, ROWS)
+            for half in TREE_HALVES:
+                nc.gpsimd.tensor_tensor(
+                    out=leaves[:, 0 : len(rows), 0:half, later],
+                    in0=leaves[:, 0 : len(rows), 0:half, later],
+                    in1=leaves[:, 0 : len(rows), half : 2 * half, later],
+                    op=ALU.add,
+                )
+
+        def exponentials(rows, acc, leaves):
+            e = work.tile([P, ROWS_PER_STEP, ROWS], F32, name="e")
+            for n in chain_rows(rows):
+                later = slice(n + 1, ROWS)
+                nc.scalar.activation(
+                    out=e[:, n % ROWS_PER_STEP, later],
+                    in_=acc[:, n % ROWS_PER_STEP, later],
+                    func=ACT.Exp,
+                    bias=k_sum[:, n : n + 1],
+                    scale=-2.0,
+                    accum_out=from_later[:, n : n + 1],
+                )
+            for r, n in enumerate(tree_rows(rows)):
+                later = slice(n + 1, ROWS)
+                nc.scalar.activation(
+                    out=e[:, n % ROWS_PER_STEP, later],
+                    in_=leaves[:, r, 0, later],
+                    func=ACT.Exp,
+                    scale=-1.0,
+                    accum_out=from_later[:, n : n + 1],
+                )
+            return e
+
+        def add_to_later_rows(rows, e):
+            for n in rows:
+                later = slice(n + 1, ROWS)
+                engine = nc.gpsimd if n in tree_rows(rows) else nc.vector
+                engine.tensor_tensor(
+                    out=from_earlier[:, n % ROWS_PER_STEP, later],
+                    in0=from_earlier[:, n % ROWS_PER_STEP, later],
+                    in1=e[:, n % ROWS_PER_STEP, later],
+                    op=ALU.add,
+                )
+
+        leaves_ahead = absolute_differences(tree_rows(steps[0]))
+
+        x_f32 = work.tile([P, ROW_BLOCKS * IN_F], F32, name="x_f32", bufs=1)
+        nc.scalar.copy(out=x_f32[:], in_=x_rows[:])
+        nc.sync.dma_start(
+            out=out[:, 0:IN_F].rearrange("(b p) i -> p b i", p=P),
+            in_=x_f32[:].rearrange("p (b i) -> p b i", b=ROW_BLOCKS),
+        )
+
+        pending = None
+        for index, rows in enumerate(steps):
+            leaves = leaves_ahead
+            if index + 1 < len(steps):
+                leaves_ahead = absolute_differences(tree_rows(steps[index + 1]))
+            acc = chains(chain_rows(rows))
+            add_tree(tree_rows(rows), leaves)
+            if pending is not None:
+                add_to_later_rows(*pending)
+            pending = (rows, exponentials(rows, acc, leaves))
+        add_to_later_rows(*pending)
+
+        nc.vector.tensor_reduce(
+            out=diversity[:], in_=from_earlier[:].rearrange("p s n -> p n s"), axis=AXIS.X, op=ALU.add
+        )
+        nc.vector.scalar_tensor_tensor(
+            out=diversity[:],
+            in0=diversity[:],
+            scalar=1.0,
+            in1=from_later[:],
+            op0=ALU.add,
+            op1=ALU.add,
+        )
+        d_t = banks.tile([P, ROW_BLOCKS, J], F32, name="d_t", tag="bank0")
+        for b in range(ROW_BLOCKS):
+            nc.tensor.transpose(d_t[:, b, :], diversity[:, b * P : (b + 1) * P], identity[:])
+        nc.vector.tensor_copy(out=d_rows[:], in_=d_t[:])
+        nc.sync.dma_start(
+            out=out[:, IN_F : IN_F + J].rearrange("(b p) j -> p b j", p=P), in_=d_rows[:]
+        )

@@ -27,9 +27,14 @@ COL_BLOCKS = COLS // BANK
 J_PER_BLOCK = BANK // K
 K_PER_BANK = BANK // ROWS
 F_BANKS = K // K_PER_BANK
-ROWS_PER_STEP = 6
-TREE_ROWS_PER_STEP = ROWS_PER_STEP // 3
-TREE_HALVES = (8, 4, 2, 1)
+WINDOW = P
+WRAPPED = ROWS + WINDOW
+VECTOR_K = range(0, 7)
+SCALAR_K = range(7, 12)
+POOL_K = range(12, 16)
+MAX_K = len(VECTOR_K) + len(POOL_K)
+QUAD = BANK // J
+HUGE = 3.0e38
 
 FLOPS = 2 * ROWS * IN_F * COLS
 
@@ -51,14 +56,25 @@ def tile_minibatchdiscriminator_kernel(tc, tensor, T, out):
             in_=tensor.rearrange("(b p) i -> p b i", p=P),
         )
 
-        f_sbuf = keep.tile([P, K, ROWS], F32)
-        f_banks = []
-        k_sum = keep.tile([P, ROWS], F32)
-        chain_start = keep.tile([P, ROWS], F32)
-        from_later = keep.tile([P, ROWS], F32)
-        from_earlier = keep.tile([P, ROWS_PER_STEP, ROWS], F32)
+        f_sbuf = keep.tile([P, K, WRAPPED], F32)
+        f_rows = [keep.tile([P, K, J], F32, name="f_rows%d" % b) for b in range(ROW_BLOCKS)]
+        half_sum = keep.tile([P, WRAPPED], F32)
+        minus_half_sum = keep.tile([P, WRAPPED], F32)
+        zeros = keep.tile([P, P], F32)
+        near = keep.tile([P, 1], F32)
         diversity = keep.tile([P, ROWS], F32)
         d_rows = keep.tile([P, ROW_BLOCKS, J], F32)
+
+        nc.vector.memset(zeros[:], 0.0)
+        nc.vector.memset(diversity[:], 1.0)
+        nc.vector.tensor_scalar(
+            out=near[:],
+            in0=identity[:, P - 1 : P],
+            scalar1=-1.0,
+            scalar2=1.0,
+            op0=ALU.mult,
+            op1=ALU.add,
+        )
 
         with tc.tile_pool(name="stage", bufs=1) as stage:
             t_raw = []
@@ -70,6 +86,15 @@ def tile_minibatchdiscriminator_kernel(tc, tensor, T, out):
                         out=raw[:, 2 * u : 2 * u + 2, :], in_=rows[:, 2 * u : 2 * u + 2, :]
                     )
                 t_raw.append(raw)
+
+            x_f32 = stage.tile([P, ROW_BLOCKS * IN_F], F32)
+            nc.gpsimd.tensor_scalar(
+                out=x_f32[:], in0=x_rows[:], scalar1=1.0, scalar2=1.0, op0=ALU.mult, op1=ALU.mult
+            )
+            nc.sync.dma_start(
+                out=out[:, 0:IN_F].rearrange("(b p) i -> p b i", p=P),
+                in_=x_f32[:].rearrange("p (b i) -> p b i", b=ROW_BLOCKS),
+            )
 
             x_words = x_rows[:].bitcast(F32)
             words_per_row = IN_F // 2
@@ -154,7 +179,6 @@ def tile_minibatchdiscriminator_kernel(tc, tensor, T, out):
                 waiting = (grouped, g, c)
             quantise_and_multiply(*waiting)
 
-            f_rows = [stage.tile([P, K, J], F32, name="f_rows%d" % b) for b in range(ROW_BLOCKS)]
             for b in range(ROW_BLOCKS):
                 for c in range(COL_BLOCKS):
                     copy = nc.vector.tensor_copy if c % 2 == 0 else nc.scalar.copy
@@ -162,143 +186,193 @@ def tile_minibatchdiscriminator_kernel(tc, tensor, T, out):
                         out=f_rows[b][:, :, c * J_PER_BLOCK : (c + 1) * J_PER_BLOCK],
                         in_=feats[b][c][:].rearrange("p (j k) -> p k j", k=K),
                     )
-            for q in range(F_BANKS):
-                f_bank = banks.tile([P, K_PER_BANK, ROWS], F32, name="f_bank%d" % q, tag="bank%d" % q)
-                for h in range(K_PER_BANK):
-                    for b in range(ROW_BLOCKS):
-                        nc.tensor.transpose(
-                            f_bank[:, h, b * P : (b + 1) * P],
-                            f_rows[b][:, K_PER_BANK * q + h, :],
-                            identity[:],
-                        )
-                copy = nc.vector.tensor_copy if q % 2 == 0 else nc.scalar.copy
-                copy(out=f_sbuf[:, K_PER_BANK * q : K_PER_BANK * (q + 1), :], in_=f_bank[:])
-                f_banks.append(f_bank)
+
+        def turn(q, order):
+            f_bank = banks.tile(
+                [P, K_PER_BANK, ROWS], F32, name="f_bank%d_%d" % (q, order[0]), tag="bank%d" % q
+            )
+            for h in range(K_PER_BANK):
+                for place, b in enumerate(order):
+                    nc.tensor.transpose(
+                        f_bank[:, h, place * P : (place + 1) * P],
+                        f_rows[b][:, K_PER_BANK * q + h, :],
+                        identity[:],
+                    )
+            return f_bank
+
+        f_banks = [turn(q, (0, 1)) for q in range(F_BANKS)]
+        for k in range(K):
+            f_k = f_banks[k // K_PER_BANK][:, k % K_PER_BANK, :]
+            if k in SCALAR_K:
+                nc.vector.tensor_scalar_mul(out=f_sbuf[:, k, 0:ROWS], in0=f_k, scalar1=0.5)
+            else:
+                nc.scalar.copy(out=f_sbuf[:, k, 0:ROWS], in_=f_k)
+        nc.vector.tensor_copy(out=f_sbuf[:, :, ROWS:WRAPPED], in_=f_sbuf[:, :, 0:WINDOW])
 
         work = pools.enter_context(tc.tile_pool(name="work", bufs=3))
 
-        nc.vector.tensor_reduce(
-            out=k_sum[:], in_=f_sbuf[:].rearrange("p k n -> p n k"), axis=AXIS.X, op=ALU.add
-        )
-        nc.vector.tensor_scalar_mul(out=chain_start[:], in0=k_sum[:], scalar1=-0.5)
-        nc.vector.memset(from_later[:], 0.0)
-        nc.vector.memset(from_earlier[:], 0.0)
+        max_sum = work.tile([P, ROWS], F32, name="max_sum", bufs=1)
+        pool_sum = work.tile([P, ROWS], F32, name="pool_sum", bufs=1)
+        for total, ks in ((max_sum, VECTOR_K), (pool_sum, POOL_K)):
+            nc.vector.tensor_reduce(
+                out=total[:],
+                in_=f_sbuf[:, ks[0] : ks[-1] + 1, 0:ROWS].rearrange("p k n -> p n k"),
+                axis=AXIS.X,
+                op=ALU.add,
+            )
+        nc.vector.tensor_tensor(out=max_sum[:], in0=max_sum[:], in1=pool_sum[:], op=ALU.add)
+        for first, last in ((0, ROWS), (ROWS, WRAPPED)):
+            nc.vector.tensor_scalar_mul(
+                out=half_sum[:, first:last], in0=max_sum[:, 0 : last - first], scalar1=0.5
+            )
+            nc.vector.tensor_scalar_mul(
+                out=minus_half_sum[:, first:last], in0=max_sum[:, 0 : last - first], scalar1=-0.5
+            )
 
-        steps = [
-            list(range(first, min(first + ROWS_PER_STEP, ROWS - 1)))
-            for first in range(0, ROWS - 1, ROWS_PER_STEP)
-        ]
+        def window(n):
+            return slice(n + 1, n + 1 + WINDOW)
 
-        def chain_rows(rows):
-            return [n for n in rows if n % 3 != 2]
-
-        def tree_rows(rows):
-            return [n for n in rows if n % 3 == 2]
-
-        def chains(rows):
-            acc = work.tile([P, ROWS_PER_STEP, ROWS], F32, name="acc")
-            for k in range(K):
-                for n in rows:
-                    later = slice(n + 1, ROWS)
-                    nc.vector.scalar_tensor_tensor(
-                        out=acc[:, n % ROWS_PER_STEP, later],
-                        in0=f_banks[k // K_PER_BANK][:, k % K_PER_BANK, later],
-                        scalar=f_sbuf[:, k, n : n + 1],
-                        in1=chain_start[:, later] if k == 0 else acc[:, n % ROWS_PER_STEP, later],
-                        op0=ALU.max,
-                        op1=ALU.add,
-                    )
+        def chains(rows, f_banks, base):
+            acc = work.tile([P, QUAD, WINDOW], F32, name="acc")
+            for k in VECTOR_K:
+                for i, n in enumerate(rows):
+                    f_k = f_banks[k // K_PER_BANK][:, k % K_PER_BANK, n + 1 - base : n + 1 - base + WINDOW]
+                    if k == VECTOR_K[0]:
+                        nc.vector.tensor_scalar(
+                            out=acc[:, i, :],
+                            in0=f_k,
+                            scalar1=f_sbuf[:, k, n : n + 1],
+                            scalar2=half_sum[:, n : n + 1],
+                            op0=ALU.max,
+                            op1=ALU.subtract,
+                        )
+                    else:
+                        nc.vector.scalar_tensor_tensor(
+                            out=acc[:, i, :],
+                            in0=f_k,
+                            scalar=f_sbuf[:, k, n : n + 1],
+                            in1=acc[:, i, :],
+                            op0=ALU.max,
+                            op1=ALU.add,
+                        )
             return acc
 
-        def absolute_differences(rows):
-            leaves = work.tile([P, TREE_ROWS_PER_STEP, K, ROWS], F32, name="leaves", bufs=2)
-            later = slice(rows[0] + 1, ROWS)
-            for r, n in enumerate(rows):
-                for k in range(K):
+        def scalar_leaves(rows):
+            leaves = work.tile([P, QUAD, len(SCALAR_K), WINDOW], F32, name="scalar_leaves")
+            for i, n in enumerate(rows):
+                for h, k in enumerate(SCALAR_K):
                     nc.scalar.activation(
-                        out=leaves[:, r, k, later],
-                        in_=f_sbuf[:, k, later],
+                        out=leaves[:, i, h, :],
+                        in_=f_sbuf[:, k, window(n)],
                         func=ACT.Abs,
                         bias=f_sbuf[:, k, n : n + 1],
                         scale=-1.0,
                     )
             return leaves
 
-        def add_tree(rows, leaves):
-            later = slice(rows[0] + 1, ROWS)
-            for half in TREE_HALVES:
-                nc.gpsimd.tensor_tensor(
-                    out=leaves[:, 0 : len(rows), 0:half, later],
-                    in0=leaves[:, 0 : len(rows), 0:half, later],
-                    in1=leaves[:, 0 : len(rows), half : 2 * half, later],
-                    op=ALU.add,
-                )
+        def pool_leaves(rows):
+            leaves = work.tile([P, QUAD, len(POOL_K), WINDOW], F32, name="pool_leaves")
+            for i, n in enumerate(rows):
+                for h, k in enumerate(POOL_K):
+                    nc.gpsimd.tensor_scalar(
+                        out=leaves[:, i, h, :],
+                        in0=f_sbuf[:, k, window(n)],
+                        scalar1=HUGE,
+                        scalar2=f_sbuf[:, k, n : n + 1],
+                        op0=ALU.min,
+                        op1=ALU.max,
+                    )
+            return leaves
 
-        def exponentials(rows, acc, leaves):
-            e = work.tile([P, ROWS_PER_STEP, ROWS], F32, name="e")
-            for n in chain_rows(rows):
-                later = slice(n + 1, ROWS)
-                nc.scalar.activation(
-                    out=e[:, n % ROWS_PER_STEP, later],
-                    in_=acc[:, n % ROWS_PER_STEP, later],
-                    func=ACT.Exp,
-                    bias=k_sum[:, n : n + 1],
-                    scale=-2.0,
-                    accum_out=from_later[:, n : n + 1],
-                )
-            for r, n in enumerate(tree_rows(rows)):
-                later = slice(n + 1, ROWS)
-                nc.scalar.activation(
-                    out=e[:, n % ROWS_PER_STEP, later],
-                    in_=leaves[:, r, 0, later],
-                    func=ACT.Exp,
-                    scale=-1.0,
-                    accum_out=from_later[:, n : n + 1],
-                )
+        def add_up(rows, acc, by_scalar, by_pool, parity):
+            half = banks.tile([P, QUAD, J], F32, name="half", tag="bank%d" % (4 + parity))
+            for i, n in enumerate(rows):
+                summands = [minus_half_sum[:, window(n)]]
+                summands += [by_scalar[:, i, h, :] for h in range(len(SCALAR_K))]
+                summands += [by_pool[:, i, h, :] for h in range(len(POOL_K))]
+                summands.append(acc[:, i, :])
+                for s, summand in enumerate(summands):
+                    nc.tensor.matmul(
+                        out=half[:, i, :],
+                        lhsT=summand,
+                        rhs=identity[:],
+                        is_transpose=True,
+                        start=(s == 0),
+                        stop=(s == len(summands) - 1),
+                    )
+            return half
+
+        def exponentials(half):
+            e = work.tile([P, QUAD, J], F32, name="e")
+            nc.scalar.activation(
+                out=e[:].rearrange("p i j -> p (i j)"),
+                in_=half[:].rearrange("p i j -> p (i j)"),
+                func=ACT.Exp,
+                scale=-2.0,
+            )
             return e
 
-        def add_to_later_rows(rows, e):
-            for n in rows:
-                later = slice(n + 1, ROWS)
-                engine = nc.gpsimd if n in tree_rows(rows) else nc.vector
-                engine.tensor_tensor(
-                    out=from_earlier[:, n % ROWS_PER_STEP, later],
-                    in0=from_earlier[:, n % ROWS_PER_STEP, later],
-                    in1=e[:, n % ROWS_PER_STEP, later],
-                    op=ALU.add,
+        own = banks.tile([P, ROWS], F32, name="own", tag="bank7")
+
+        def add_to_sums(rows, e, base, to_others, last):
+            for i, n in enumerate(rows):
+                place = n - base if (n - base) % 2 == 0 else ROWS + n - base + 1
+                nc.tensor.matmul(
+                    out=to_others[:, place : place + WINDOW],
+                    lhsT=e[:, i, :],
+                    rhs=identity[:],
+                    is_transpose=True,
+                    start=False,
+                    stop=(last and i == len(rows) - 1),
+                )
+            for i, n in enumerate(rows):
+                nc.tensor.matmul(
+                    out=own[:, n : n + 1], lhsT=e[:, i, :], rhs=near[:], start=True, stop=True
                 )
 
-        leaves_ahead = absolute_differences(tree_rows(steps[0]))
+        HALF_STEPS = P // QUAD
+        for base in (0, P):
+            if base:
+                f_banks = [turn(q, (1, 0)) for q in range((len(VECTOR_K) + 1) // K_PER_BANK)]
+            to_others = banks.tile([P, 2 * ROWS], F32, name="to_others%d" % base, tag="bank6")
+            for piece in range(2 * ROWS // P):
+                nc.tensor.matmul(
+                    out=to_others[:, piece * P : (piece + 1) * P],
+                    lhsT=zeros[:],
+                    rhs=identity[:],
+                    is_transpose=True,
+                    start=(piece == 0),
+                    stop=False,
+                )
+            made = {}
+            summed = {}
+            for t in range(HALF_STEPS + 2):
+                if t < HALF_STEPS:
+                    rows = list(range(base + QUAD * t, base + QUAD * (t + 1)))
+                    made[t] = (rows, chains(rows, f_banks, base), scalar_leaves(rows), pool_leaves(rows))
+                if 0 <= t - 1 < HALF_STEPS:
+                    rows, acc, by_scalar, by_pool = made[t - 1]
+                    half = add_up(rows, acc, by_scalar, by_pool, (t - 1) % 2)
+                    summed[t - 1] = (rows, exponentials(half))
+                if 0 <= t - 2 < HALF_STEPS:
+                    rows, e = summed[t - 2]
+                    add_to_sums(rows, e, base, to_others, t - 2 == HALF_STEPS - 1)
+            for shift, first in ((1, 0), (0, ROWS)):
+                width = ROWS - 1 if shift else ROWS
+                pieces = [(base + shift, first, width)]
+                if base:
+                    wrap = ROWS - base - shift
+                    pieces = [(base + shift, first, wrap), (0, first + wrap, width - wrap)]
+                for row, column, count in pieces:
+                    nc.vector.tensor_tensor(
+                        out=diversity[:, row : row + count],
+                        in0=to_others[:, column : column + count],
+                        in1=diversity[:, row : row + count],
+                        op=ALU.add,
+                    )
 
-        x_f32 = work.tile([P, ROW_BLOCKS * IN_F], F32, name="x_f32", bufs=1)
-        nc.scalar.copy(out=x_f32[:], in_=x_rows[:])
-        nc.sync.dma_start(
-            out=out[:, 0:IN_F].rearrange("(b p) i -> p b i", p=P),
-            in_=x_f32[:].rearrange("p (b i) -> p b i", b=ROW_BLOCKS),
-        )
-
-        pending = None
-        for index, rows in enumerate(steps):
-            leaves = leaves_ahead
-            if index + 1 < len(steps):
-                leaves_ahead = absolute_differences(tree_rows(steps[index + 1]))
-            acc = chains(chain_rows(rows))
-            add_tree(tree_rows(rows), leaves)
-            if pending is not None:
-                add_to_later_rows(*pending)
-            pending = (rows, exponentials(rows, acc, leaves))
-        add_to_later_rows(*pending)
-
-        nc.vector.tensor_reduce(
-            out=diversity[:], in_=from_earlier[:].rearrange("p s n -> p n s"), axis=AXIS.X, op=ALU.add
-        )
-        nc.vector.scalar_tensor_tensor(
-            out=diversity[:],
-            in0=diversity[:],
-            scalar=1.0,
-            in1=from_later[:],
-            op0=ALU.add,
-            op1=ALU.add,
+        nc.vector.tensor_tensor(
+            out=diversity[:], in0=own[:], in1=diversity[:], op=ALU.add
         )
         d_t = banks.tile([P, ROW_BLOCKS, J], F32, name="d_t", tag="bank0")
         for b in range(ROW_BLOCKS):

@@ -29,12 +29,9 @@ K_PER_BANK = BANK // ROWS
 F_BANKS = K // K_PER_BANK
 WINDOW = P
 WRAPPED = ROWS + WINDOW
-VECTOR_K = range(0, 7)
-SCALAR_K = range(7, 12)
-POOL_K = range(12, 16)
-MAX_K = len(VECTOR_K) + len(POOL_K)
+VECTOR_K = range(0, 8)
+SCALAR_K = range(8, 16)
 QUAD = BANK // J
-HUGE = 3.0e38
 
 FLOPS = 2 * ROWS * IN_F * COLS
 
@@ -212,15 +209,12 @@ def tile_minibatchdiscriminator_kernel(tc, tensor, T, out):
         work = pools.enter_context(tc.tile_pool(name="work", bufs=3))
 
         max_sum = work.tile([P, ROWS], F32, name="max_sum", bufs=1)
-        pool_sum = work.tile([P, ROWS], F32, name="pool_sum", bufs=1)
-        for total, ks in ((max_sum, VECTOR_K), (pool_sum, POOL_K)):
-            nc.vector.tensor_reduce(
-                out=total[:],
-                in_=f_sbuf[:, ks[0] : ks[-1] + 1, 0:ROWS].rearrange("p k n -> p n k"),
-                axis=AXIS.X,
-                op=ALU.add,
-            )
-        nc.vector.tensor_tensor(out=max_sum[:], in0=max_sum[:], in1=pool_sum[:], op=ALU.add)
+        nc.vector.tensor_reduce(
+            out=max_sum[:],
+            in_=f_sbuf[:, 0 : len(VECTOR_K), 0:ROWS].rearrange("p k n -> p n k"),
+            axis=AXIS.X,
+            op=ALU.add,
+        )
         for first, last in ((0, ROWS), (ROWS, WRAPPED)):
             nc.vector.tensor_scalar_mul(
                 out=half_sum[:, first:last], in0=max_sum[:, 0 : last - first], scalar1=0.5
@@ -270,26 +264,11 @@ def tile_minibatchdiscriminator_kernel(tc, tensor, T, out):
                     )
             return leaves
 
-        def pool_leaves(rows):
-            leaves = work.tile([P, QUAD, len(POOL_K), WINDOW], F32, name="pool_leaves")
-            for i, n in enumerate(rows):
-                for h, k in enumerate(POOL_K):
-                    nc.gpsimd.tensor_scalar(
-                        out=leaves[:, i, h, :],
-                        in0=f_sbuf[:, k, window(n)],
-                        scalar1=HUGE,
-                        scalar2=f_sbuf[:, k, n : n + 1],
-                        op0=ALU.min,
-                        op1=ALU.max,
-                    )
-            return leaves
-
-        def add_up(rows, acc, by_scalar, by_pool, parity):
+        def add_up(rows, acc, by_scalar, parity):
             half = banks.tile([P, QUAD, J], F32, name="half", tag="bank%d" % (4 + parity))
             for i, n in enumerate(rows):
                 summands = [minus_half_sum[:, window(n)]]
                 summands += [by_scalar[:, i, h, :] for h in range(len(SCALAR_K))]
-                summands += [by_pool[:, i, h, :] for h in range(len(POOL_K))]
                 summands.append(acc[:, i, :])
                 for s, summand in enumerate(summands):
                     nc.tensor.matmul(
@@ -349,10 +328,10 @@ def tile_minibatchdiscriminator_kernel(tc, tensor, T, out):
             for t in range(HALF_STEPS + 2):
                 if t < HALF_STEPS:
                     rows = list(range(base + QUAD * t, base + QUAD * (t + 1)))
-                    made[t] = (rows, chains(rows, f_banks, base), scalar_leaves(rows), pool_leaves(rows))
+                    made[t] = (rows, chains(rows, f_banks, base), scalar_leaves(rows))
                 if 0 <= t - 1 < HALF_STEPS:
-                    rows, acc, by_scalar, by_pool = made[t - 1]
-                    half = add_up(rows, acc, by_scalar, by_pool, (t - 1) % 2)
+                    rows, acc, by_scalar = made[t - 1]
+                    half = add_up(rows, acc, by_scalar, (t - 1) % 2)
                     summed[t - 1] = (rows, exponentials(half))
                 if 0 <= t - 2 < HALF_STEPS:
                     rows, e = summed[t - 2]

@@ -55,6 +55,10 @@ def tile_minibatchdiscriminator_kernel(tc, tensor, T, out):
 
         f_sbuf = keep.tile([P, K, WRAPPED], F32)
         f_rows = [keep.tile([P, K, J], F32, name="f_rows%d" % b) for b in range(ROW_BLOCKS)]
+        x_codes = keep.tile([P, PASSES, ROWS], U32, align_bytes=64)
+        x_scales = keep.tile([P, PASSES, ROWS], U8, align_bytes=64)
+        t_codes = keep.tile([P, PASSES, COLS], U32, align_bytes=64)
+        t_scales = keep.tile([P, PASSES, COLS], U8, align_bytes=64)
         half_sum = keep.tile([P, WRAPPED], F32)
         minus_half_sum = keep.tile([P, WRAPPED], F32)
         zeros = keep.tile([P, P], F32)
@@ -112,16 +116,12 @@ def tile_minibatchdiscriminator_kernel(tc, tensor, T, out):
                 nc.vector.tensor_copy(
                     out=x_grouped_words[:, g], in_=x_t[:].rearrange("p u n -> p n u")
                 )
-            x_codes = stage.tile([P, PASSES, ROWS], U32, align_bytes=64)
-            x_scales = stage.tile([P, PASSES, ROWS], U8, align_bytes=64)
             nc.vector.quantize_mx(
                 out=x_codes[:].rearrange("p g n -> p (g n)").bitcast(FP8X4),
                 scales=x_scales[:].rearrange("p g n -> p (g n)"),
                 in_=x_grouped[:],
             )
 
-            t_codes = stage.tile([P, PASSES, COLS], U32, align_bytes=64)
-            t_scales = stage.tile([P, PASSES, COLS], U8, align_bytes=64)
             feats = [
                 [
                     banks.tile(
@@ -266,6 +266,15 @@ def tile_minibatchdiscriminator_kernel(tc, tensor, T, out):
 
         def add_up(rows, acc, by_scalar, parity):
             half = banks.tile([P, QUAD, J], F32, name="half", tag="bank%d" % (4 + parity))
+            nc.tensor.matmul_mx(
+                out=half[:].rearrange("p i j -> p (i j)"),
+                lhsT=x_codes[:, 0, 0:P].bitcast(FP8X4),
+                lhsT_scale=x_scales[:, 0, 0:P],
+                rhs=t_codes[:, 0, 0:BANK].bitcast(FP8X4),
+                rhs_scale=t_scales[:, 0, 0:BANK],
+                start=True,
+                stop=True,
+            )
             for i, n in enumerate(rows):
                 summands = [minus_half_sum[:, window(n)]]
                 summands += [by_scalar[:, i, h, :] for h in range(len(SCALAR_K))]

@@ -31,6 +31,7 @@ WINDOW = P
 WRAPPED = ROWS + WINDOW
 VECTOR_K = range(0, 8)
 SCALAR_K = range(8, 16)
+WAKE_PASSES = 3
 QUAD = BANK // J
 
 FLOPS = 2 * ROWS * IN_F * COLS
@@ -266,15 +267,16 @@ def tile_minibatchdiscriminator_kernel(tc, tensor, T, out):
 
         def add_up(rows, acc, by_scalar, parity):
             half = banks.tile([P, QUAD, J], F32, name="half", tag="bank%d" % (4 + parity))
-            nc.tensor.matmul_mx(
-                out=half[:].rearrange("p i j -> p (i j)"),
-                lhsT=x_codes[:, 0, 0:P].bitcast(FP8X4),
-                lhsT_scale=x_scales[:, 0, 0:P],
-                rhs=t_codes[:, 0, 0:BANK].bitcast(FP8X4),
-                rhs_scale=t_scales[:, 0, 0:BANK],
-                start=True,
-                stop=True,
-            )
+            for g in range(WAKE_PASSES):
+                nc.tensor.matmul_mx(
+                    out=half[:].rearrange("p i j -> p (i j)"),
+                    lhsT=x_codes[:, g, 0:P].bitcast(FP8X4),
+                    lhsT_scale=x_scales[:, g, 0:P],
+                    rhs=t_codes[:, g, 0:BANK].bitcast(FP8X4),
+                    rhs_scale=t_scales[:, g, 0:BANK],
+                    start=(g == 0),
+                    stop=(g == WAKE_PASSES - 1),
+                )
             for i, n in enumerate(rows):
                 summands = [minus_half_sum[:, window(n)]]
                 summands += [by_scalar[:, i, h, :] for h in range(len(SCALAR_K))]

@@ -29,9 +29,12 @@ K_PER_BANK = BANK // ROWS
 F_BANKS = K // K_PER_BANK
 WINDOW = P
 WRAPPED = ROWS + WINDOW
-VECTOR_K = range(0, 8)
-SCALAR_K = range(8, 16)
+CHAIN_K = range(0, 5)
+LONE_K = range(5, 9)
+SCALAR_K = range(9, 16)
+MAX_K = range(0, 9)
 WAKE_PASSES = 3
+WAKE_EVERY = 2
 QUAD = BANK // J
 
 FLOPS = 2 * ROWS * IN_F * COLS
@@ -60,23 +63,15 @@ def tile_minibatchdiscriminator_kernel(tc, tensor, T, out):
         x_scales = keep.tile([P, PASSES, ROWS], U8, align_bytes=64)
         t_codes = keep.tile([P, PASSES, COLS], U32, align_bytes=64)
         t_scales = keep.tile([P, PASSES, COLS], U8, align_bytes=64)
-        half_sum = keep.tile([P, WRAPPED], F32)
+        half_sum = keep.tile([P, ROWS], F32)
         minus_half_sum = keep.tile([P, WRAPPED], F32)
         zeros = keep.tile([P, P], F32)
-        near = keep.tile([P, 1], F32)
+        from_later = keep.tile([P, ROWS], F32)
         diversity = keep.tile([P, ROWS], F32)
         d_rows = keep.tile([P, ROW_BLOCKS, J], F32)
 
         nc.vector.memset(zeros[:], 0.0)
         nc.vector.memset(diversity[:], 1.0)
-        nc.vector.tensor_scalar(
-            out=near[:],
-            in0=identity[:, P - 1 : P],
-            scalar1=-1.0,
-            scalar2=1.0,
-            op0=ALU.mult,
-            op1=ALU.add,
-        )
 
         with tc.tile_pool(name="stage", bufs=1) as stage:
             t_raw = []
@@ -207,54 +202,73 @@ def tile_minibatchdiscriminator_kernel(tc, tensor, T, out):
                 nc.scalar.copy(out=f_sbuf[:, k, 0:ROWS], in_=f_k)
         nc.vector.tensor_copy(out=f_sbuf[:, :, ROWS:WRAPPED], in_=f_sbuf[:, :, 0:WINDOW])
 
-        work = pools.enter_context(tc.tile_pool(name="work", bufs=3))
-
-        max_sum = work.tile([P, ROWS], F32, name="max_sum", bufs=1)
-        nc.vector.tensor_reduce(
-            out=max_sum[:],
-            in_=f_sbuf[:, 0 : len(VECTOR_K), 0:ROWS].rearrange("p k n -> p n k"),
-            axis=AXIS.X,
-            op=ALU.add,
-        )
+        max_sum = banks.tile([P, ROWS], F32, name="max_sum", tag="bank7")
+        for b in range(ROW_BLOCKS):
+            for k in MAX_K:
+                nc.tensor.matmul(
+                    out=max_sum[:, b * P : (b + 1) * P],
+                    lhsT=f_rows[b][:, k, :],
+                    rhs=identity[:],
+                    is_transpose=True,
+                    start=(k == MAX_K[0]),
+                    stop=(k == MAX_K[-1]),
+                )
+        nc.vector.tensor_scalar_mul(out=half_sum[:], in0=max_sum[:], scalar1=0.5)
         for first, last in ((0, ROWS), (ROWS, WRAPPED)):
-            nc.vector.tensor_scalar_mul(
-                out=half_sum[:, first:last], in0=max_sum[:, 0 : last - first], scalar1=0.5
-            )
             nc.vector.tensor_scalar_mul(
                 out=minus_half_sum[:, first:last], in0=max_sum[:, 0 : last - first], scalar1=-0.5
             )
 
+        work = pools.enter_context(tc.tile_pool(name="work", bufs=3))
+
+        def rows_of(quad):
+            return range(QUAD * quad, QUAD * (quad + 1))
+
+        def base_of(quad):
+            return rows_of(quad)[0] // P * P
+
         def window(n):
             return slice(n + 1, n + 1 + WINDOW)
 
-        def chains(rows, f_banks, base):
-            acc = work.tile([P, QUAD, WINDOW], F32, name="acc")
-            for k in VECTOR_K:
-                for i, n in enumerate(rows):
-                    f_k = f_banks[k // K_PER_BANK][:, k % K_PER_BANK, n + 1 - base : n + 1 - base + WINDOW]
-                    if k == VECTOR_K[0]:
+        def lone_maxima(quad):
+            leaves = work.tile([P, QUAD, len(LONE_K), WINDOW], F32, name="lone")
+            for i, n in enumerate(rows_of(quad)):
+                for h, k in enumerate(LONE_K):
+                    if h == 0:
                         nc.vector.tensor_scalar(
-                            out=acc[:, i, :],
-                            in0=f_k,
+                            out=leaves[:, i, h, :],
+                            in0=f_sbuf[:, k, window(n)],
                             scalar1=f_sbuf[:, k, n : n + 1],
                             scalar2=half_sum[:, n : n + 1],
                             op0=ALU.max,
                             op1=ALU.subtract,
                         )
                     else:
-                        nc.vector.scalar_tensor_tensor(
-                            out=acc[:, i, :],
-                            in0=f_k,
-                            scalar=f_sbuf[:, k, n : n + 1],
-                            in1=acc[:, i, :],
-                            op0=ALU.max,
-                            op1=ALU.add,
+                        nc.vector.tensor_scalar_max(
+                            out=leaves[:, i, h, :],
+                            in0=f_sbuf[:, k, window(n)],
+                            scalar1=f_sbuf[:, k, n : n + 1],
                         )
+            return leaves
+
+        def chains(quad, f_banks):
+            acc = work.tile([P, QUAD, WINDOW], F32, name="acc")
+            for k in CHAIN_K:
+                for i, n in enumerate(rows_of(quad)):
+                    first = n + 1 - base_of(quad)
+                    nc.vector.scalar_tensor_tensor(
+                        out=acc[:, i, :],
+                        in0=f_banks[k // K_PER_BANK][:, k % K_PER_BANK, first : first + WINDOW],
+                        scalar=f_sbuf[:, k, n : n + 1],
+                        in1=minus_half_sum[:, window(n)] if k == CHAIN_K[0] else acc[:, i, :],
+                        op0=ALU.max,
+                        op1=ALU.add,
+                    )
             return acc
 
-        def scalar_leaves(rows):
+        def absolute_differences(quad):
             leaves = work.tile([P, QUAD, len(SCALAR_K), WINDOW], F32, name="scalar_leaves")
-            for i, n in enumerate(rows):
+            for i, n in enumerate(rows_of(quad)):
                 for h, k in enumerate(SCALAR_K):
                     nc.scalar.activation(
                         out=leaves[:, i, h, :],
@@ -265,20 +279,21 @@ def tile_minibatchdiscriminator_kernel(tc, tensor, T, out):
                     )
             return leaves
 
-        def add_up(rows, acc, by_scalar, parity):
-            half = banks.tile([P, QUAD, J], F32, name="half", tag="bank%d" % (4 + parity))
-            for g in range(WAKE_PASSES):
-                nc.tensor.matmul_mx(
-                    out=half[:].rearrange("p i j -> p (i j)"),
-                    lhsT=x_codes[:, g, 0:P].bitcast(FP8X4),
-                    lhsT_scale=x_scales[:, g, 0:P],
-                    rhs=t_codes[:, g, 0:BANK].bitcast(FP8X4),
-                    rhs_scale=t_scales[:, g, 0:BANK],
-                    start=(g == 0),
-                    stop=(g == WAKE_PASSES - 1),
-                )
-            for i, n in enumerate(rows):
-                summands = [minus_half_sum[:, window(n)]]
+        def add_up(quad, lone, acc, by_scalar):
+            half = banks.tile([P, QUAD, J], F32, name="half", tag="bank%d" % (3 + quad % 2))
+            if quad % WAKE_EVERY == 0:
+                for g in range(WAKE_PASSES):
+                    nc.tensor.matmul_mx(
+                        out=half[:].rearrange("p i j -> p (i j)"),
+                        lhsT=x_codes[:, g, 0:P].bitcast(FP8X4),
+                        lhsT_scale=x_scales[:, g, 0:P],
+                        rhs=t_codes[:, g, 0:BANK].bitcast(FP8X4),
+                        rhs_scale=t_scales[:, g, 0:BANK],
+                        start=(g == 0),
+                        stop=(g == WAKE_PASSES - 1),
+                    )
+            for i in range(QUAD):
+                summands = [lone[:, i, h, :] for h in range(len(LONE_K))]
                 summands += [by_scalar[:, i, h, :] for h in range(len(SCALAR_K))]
                 summands.append(acc[:, i, :])
                 for s, summand in enumerate(summands):
@@ -302,67 +317,91 @@ def tile_minibatchdiscriminator_kernel(tc, tensor, T, out):
             )
             return e
 
-        own = banks.tile([P, ROWS], F32, name="own", tag="bank7")
-
-        def add_to_sums(rows, e, base, to_others, last):
-            for i, n in enumerate(rows):
-                place = n - base if (n - base) % 2 == 0 else ROWS + n - base + 1
-                nc.tensor.matmul(
-                    out=to_others[:, place : place + WINDOW],
-                    lhsT=e[:, i, :],
-                    rhs=identity[:],
-                    is_transpose=True,
-                    start=False,
-                    stop=(last and i == len(rows) - 1),
-                )
-            for i, n in enumerate(rows):
-                nc.tensor.matmul(
-                    out=own[:, n : n + 1], lhsT=e[:, i, :], rhs=near[:], start=True, stop=True
-                )
-
-        HALF_STEPS = P // QUAD
-        for base in (0, P):
-            if base:
-                f_banks = [turn(q, (1, 0)) for q in range((len(VECTOR_K) + 1) // K_PER_BANK)]
-            to_others = banks.tile([P, 2 * ROWS], F32, name="to_others%d" % base, tag="bank6")
+        def open_others(base):
+            others = banks.tile([P, 2 * ROWS], F32, name="others%d" % base, tag="bank7")
             for piece in range(2 * ROWS // P):
                 nc.tensor.matmul(
-                    out=to_others[:, piece * P : (piece + 1) * P],
+                    out=others[:, piece * P : (piece + 1) * P],
                     lhsT=zeros[:],
                     rhs=identity[:],
                     is_transpose=True,
                     start=(piece == 0),
                     stop=False,
                 )
-            made = {}
-            summed = {}
-            for t in range(HALF_STEPS + 2):
-                if t < HALF_STEPS:
-                    rows = list(range(base + QUAD * t, base + QUAD * (t + 1)))
-                    made[t] = (rows, chains(rows, f_banks, base), scalar_leaves(rows))
-                if 0 <= t - 1 < HALF_STEPS:
-                    rows, acc, by_scalar = made[t - 1]
-                    half = add_up(rows, acc, by_scalar, (t - 1) % 2)
-                    summed[t - 1] = (rows, exponentials(half))
-                if 0 <= t - 2 < HALF_STEPS:
-                    rows, e = summed[t - 2]
-                    add_to_sums(rows, e, base, to_others, t - 2 == HALF_STEPS - 1)
+            return others
+
+        def turn_back(quad, e, others, last):
+            turned = banks.tile([P, QUAD, WINDOW], F32, name="turned", tag="bank%d" % (5 + quad % 2))
+            for i in range(QUAD):
+                nc.tensor.transpose(turned[:, i, :], e[:, i, :], identity[:])
+            for i, n in enumerate(rows_of(quad)):
+                place = n - base_of(quad)
+                if place % 2 == 1:
+                    place += ROWS + 1
+                nc.tensor.matmul(
+                    out=others[:, place : place + WINDOW],
+                    lhsT=e[:, i, :],
+                    rhs=identity[:],
+                    is_transpose=True,
+                    start=False,
+                    stop=(last and i == QUAD - 1),
+                )
+            return turned
+
+        def sum_over_later(quad, turned):
+            first = QUAD * quad
+            nc.vector.tensor_reduce(
+                out=from_later[:, first : first + QUAD],
+                in_=turned[:, :, 0 : WINDOW - 1],
+                axis=AXIS.X,
+                op=ALU.add,
+            )
+
+        def add_others(others, base):
             for shift, first in ((1, 0), (0, ROWS)):
-                width = ROWS - 1 if shift else ROWS
-                pieces = [(base + shift, first, width)]
-                if base:
-                    wrap = ROWS - base - shift
-                    pieces = [(base + shift, first, wrap), (0, first + wrap, width - wrap)]
+                width = ROWS - shift
+                before_wrap = min(width, ROWS - base - shift)
+                pieces = [(base + shift, first, before_wrap)]
+                if before_wrap < width:
+                    pieces.append((0, first + before_wrap, width - before_wrap))
                 for row, column, count in pieces:
                     nc.vector.tensor_tensor(
                         out=diversity[:, row : row + count],
-                        in0=to_others[:, column : column + count],
+                        in0=others[:, column : column + count],
                         in1=diversity[:, row : row + count],
                         op=ALU.add,
                     )
 
+        QUADS = ROWS // QUAD
+        HALF = QUADS // 2
+        with tc.manual_schedule():
+            leaves = {}
+            halves = {}
+            es = {}
+            turned = {}
+            others = None
+            for t in range(QUADS + 4):
+                if t == HALF:
+                    f_banks = [turn(q, (1, 0)) for q in range((len(CHAIN_K) + 1) // K_PER_BANK)]
+                if 0 <= t - 2 < QUADS:
+                    es[t - 2] = exponentials(halves[t - 2])
+                if t < QUADS:
+                    leaves[t] = (lone_maxima(t), chains(t, f_banks), absolute_differences(t))
+                if 0 <= t - 1 < QUADS:
+                    halves[t - 1] = add_up(t - 1, *leaves[t - 1])
+                quad = t - 3
+                if 0 <= quad < QUADS:
+                    if quad % HALF == 0:
+                        others = open_others(base_of(quad))
+                    last = quad % HALF == HALF - 1
+                    turned[quad] = turn_back(quad, es[quad], others, last)
+                    if last:
+                        add_others(others, base_of(quad))
+                if 0 <= t - 4 < QUADS:
+                    sum_over_later(t - 4, turned[t - 4])
+
         nc.vector.tensor_tensor(
-            out=diversity[:], in0=own[:], in1=diversity[:], op=ALU.add
+            out=diversity[:], in0=from_later[:], in1=diversity[:], op=ALU.add
         )
         d_t = banks.tile([P, ROW_BLOCKS, J], F32, name="d_t", tag="bank0")
         for b in range(ROW_BLOCKS):

@@ -34,7 +34,7 @@ LONE_K = range(5, 9)
 SCALAR_K = range(9, 16)
 MAX_K = range(0, 9)
 WAKE_PASSES = 3
-WAKE_EVERY = 2
+WAKE_EVERY = 4
 QUAD = BANK // J
 
 FLOPS = 2 * ROWS * IN_F * COLS
@@ -292,10 +292,10 @@ def tile_minibatchdiscriminator_kernel(tc, tensor, T, out):
                         start=(g == 0),
                         stop=(g == WAKE_PASSES - 1),
                     )
-            for i in range(QUAD):
-                summands = [lone[:, i, h, :] for h in range(len(LONE_K))]
-                summands += [by_scalar[:, i, h, :] for h in range(len(SCALAR_K))]
-                summands.append(acc[:, i, :])
+            for i in reversed(range(QUAD)):
+                summands = [acc[:, i, :]]
+                summands += [by_scalar[:, i, h, :] for h in reversed(range(len(SCALAR_K)))]
+                summands += [lone[:, i, h, :] for h in reversed(range(len(LONE_K)))]
                 for s, summand in enumerate(summands):
                     nc.tensor.matmul(
                         out=half[:, i, :],

@@ -24,6 +24,8 @@ K_PASS = P * PACK
 PASSES = IN_F // K_PASS
 BANK = 512
 COL_BLOCKS = COLS // BANK
+SIDES = 2
+SIDE = COLS // SIDES
 J_PER_BLOCK = BANK // K
 K_PER_BANK = BANK // ROWS
 F_BANKS = K // K_PER_BANK
@@ -33,8 +35,8 @@ CHAIN_K = range(0, 5)
 LONE_K = range(5, 9)
 SCALAR_K = range(9, 16)
 MAX_K = range(0, 9)
-WAKE_PASSES = 3
-WAKE_EVERY = 4
+PLAIN_QUADS = 3
+QUADS_PER_ROUND = 4
 QUAD = BANK // J
 
 FLOPS = 2 * ROWS * IN_F * COLS
@@ -52,17 +54,20 @@ def tile_minibatchdiscriminator_kernel(tc, tensor, T, out):
         make_identity(nc, identity[:])
 
         x_rows = keep.tile([P, ROW_BLOCKS * IN_F], BF16)
-        nc.sync.dma_start(
-            out=x_rows[:].rearrange("p (b i) -> p b i", b=ROW_BLOCKS),
-            in_=tensor.rearrange("(b p) i -> p b i", p=P),
-        )
+        x_f32 = keep.tile([P, ROW_BLOCKS * IN_F], F32)
+        x_halves = []
+        for columns in (slice(0, IN_F // 2), slice(IN_F // 2, IN_F)):
+            half_of = [
+                tile[:].rearrange("p (b i) -> p b i", b=ROW_BLOCKS)[:, :, columns]
+                for tile in (x_rows, x_f32)
+            ]
+            nc.sync.dma_start(
+                out=half_of[0], in_=tensor.rearrange("(b p) i -> p b i", p=P)[:, :, columns]
+            )
+            x_halves.append(half_of)
 
         f_sbuf = keep.tile([P, K, WRAPPED], F32)
         f_rows = [keep.tile([P, K, J], F32, name="f_rows%d" % b) for b in range(ROW_BLOCKS)]
-        x_codes = keep.tile([P, PASSES, ROWS], U32, align_bytes=64)
-        x_scales = keep.tile([P, PASSES, ROWS], U8, align_bytes=64)
-        t_codes = keep.tile([P, PASSES, COLS], U32, align_bytes=64)
-        t_scales = keep.tile([P, PASSES, COLS], U8, align_bytes=64)
         half_sum = keep.tile([P, ROWS], F32)
         minus_half_sum = keep.tile([P, WRAPPED], F32)
         zeros = keep.tile([P, P], F32)
@@ -71,23 +76,29 @@ def tile_minibatchdiscriminator_kernel(tc, tensor, T, out):
         d_rows = keep.tile([P, ROW_BLOCKS, J], F32)
 
         nc.vector.memset(zeros[:], 0.0)
+        nc.scalar.activation(out=d_rows[:, 0, 0:1], in_=zeros[:, 0:1], func=ACT.Exp)
         nc.vector.memset(diversity[:], 1.0)
 
         with tc.tile_pool(name="stage", bufs=1) as stage:
-            t_raw = []
-            for g in range(PASSES):
-                raw = stage.tile([P, PACK, COLS], BF16, name="t_raw%d" % g)
-                rows = weights[K_PASS * g : K_PASS * (g + 1), :].rearrange("(p t) c -> p t c", t=PACK)
-                for u in range(2):
+            x_codes = stage.tile([P, PASSES, ROWS], U32, align_bytes=64)
+            x_scales = stage.tile([P, PASSES, ROWS], U8, align_bytes=64)
+            t_codes = stage.tile([P, PASSES, COLS], U32, align_bytes=64)
+            t_scales = stage.tile([P, PASSES, COLS], U8, align_bytes=64)
+            t_raw = {}
+            for side in range(SIDES):
+                columns = slice(side * SIDE, (side + 1) * SIDE)
+                for g in range(PASSES):
+                    raw = stage.tile([P, PACK, SIDE], BF16, name="t_raw%d_%d" % (g, side))
+                    rows = weights[K_PASS * g : K_PASS * (g + 1), :]
                     nc.sync.dma_start(
-                        out=raw[:, 2 * u : 2 * u + 2, :], in_=rows[:, 2 * u : 2 * u + 2, :]
+                        out=raw[:], in_=rows.rearrange("(p t) c -> p t c", t=PACK)[:, :, columns]
                     )
-                t_raw.append(raw)
+                    t_raw[g, side] = raw
 
-            x_f32 = stage.tile([P, ROW_BLOCKS * IN_F], F32)
-            nc.gpsimd.tensor_scalar(
-                out=x_f32[:], in0=x_rows[:], scalar1=1.0, scalar2=1.0, op0=ALU.mult, op1=ALU.mult
-            )
+            for source, copied in x_halves:
+                nc.gpsimd.tensor_scalar(
+                    out=copied, in0=source, scalar1=1.0, scalar2=1.0, op0=ALU.mult, op1=ALU.mult
+                )
             nc.sync.dma_start(
                 out=out[:, 0:IN_F].rearrange("(b p) i -> p b i", p=P),
                 in_=x_f32[:].rearrange("p (b i) -> p b i", b=ROW_BLOCKS),
@@ -109,14 +120,7 @@ def tile_minibatchdiscriminator_kernel(tc, tensor, T, out):
                             x_words[:, first + u : first + 2 * P : 2],
                             identity[:],
                         )
-                nc.vector.tensor_copy(
-                    out=x_grouped_words[:, g], in_=x_t[:].rearrange("p u n -> p n u")
-                )
-            nc.vector.quantize_mx(
-                out=x_codes[:].rearrange("p g n -> p (g n)").bitcast(FP8X4),
-                scales=x_scales[:].rearrange("p g n -> p (g n)"),
-                in_=x_grouped[:],
-            )
+                nc.scalar.copy(out=x_grouped_words[:, g], in_=x_t[:].rearrange("p u n -> p n u"))
 
             feats = [
                 [
@@ -133,14 +137,14 @@ def tile_minibatchdiscriminator_kernel(tc, tensor, T, out):
 
             def regroup(g, c):
                 grouped = stage.tile(
-                    [P, BANK, PACK], BF16, name="t_grouped", bufs=4, align_bytes=64
+                    [P, BANK, PACK], BF16, name="t_grouped", bufs=8, align_bytes=64
                 )
                 copy = nc.vector.tensor_copy if c % 2 == 0 else nc.scalar.copy
+                raw = t_raw[g, c * BANK // SIDE]
+                first = c * BANK % SIDE
                 copy(
                     out=grouped[:].rearrange("p (c i) t -> p c t i", i=4),
-                    in_=t_raw[g][:, :, c * BANK : (c + 1) * BANK].rearrange(
-                        "p t (c i) -> p c t i", i=4
-                    ),
+                    in_=raw[:, :, first : first + BANK].rearrange("p t (c i) -> p c t i", i=4),
                 )
                 return grouped
 
@@ -163,22 +167,33 @@ def tile_minibatchdiscriminator_kernel(tc, tensor, T, out):
                         stop=(g == PASSES - 1),
                     )
 
-            pieces = [(g, c) for g in range(PASSES) for c in range(COL_BLOCKS)]
-            waiting = None
-            for g, c in pieces:
-                grouped = regroup(g, c)
-                if waiting is not None:
-                    quantise_and_multiply(*waiting)
-                waiting = (grouped, g, c)
-            quantise_and_multiply(*waiting)
-
-            for b in range(ROW_BLOCKS):
-                for c in range(COL_BLOCKS):
-                    copy = nc.vector.tensor_copy if c % 2 == 0 else nc.scalar.copy
+            def sort_by_k(c):
+                for b in range(ROW_BLOCKS):
+                    copy = nc.vector.tensor_copy if b == 0 else nc.scalar.copy
                     copy(
                         out=f_rows[b][:, :, c * J_PER_BLOCK : (c + 1) * J_PER_BLOCK],
                         in_=feats[b][c][:].rearrange("p (j k) -> p k j", k=K),
                     )
+
+            waiting = None
+            for side in range(SIDES):
+                for g in range(PASSES):
+                    for c in range(side * SIDE // BANK, (side + 1) * SIDE // BANK):
+                        grouped = regroup(g, c)
+                        if waiting is None:
+                            nc.vector.quantize_mx(
+                                out=x_codes[:].rearrange("p g n -> p (g n)").bitcast(FP8X4),
+                                scales=x_scales[:].rearrange("p g n -> p (g n)"),
+                                in_=x_grouped[:],
+                            )
+                        else:
+                            quantise_and_multiply(*waiting)
+                        waiting = (grouped, g, c)
+                    if side == 1 and g < 2:
+                        sort_by_k(g)
+            quantise_and_multiply(*waiting)
+            sort_by_k(2)
+            sort_by_k(3)
 
         def turn(q, order):
             f_bank = banks.tile(
@@ -193,16 +208,11 @@ def tile_minibatchdiscriminator_kernel(tc, tensor, T, out):
                     )
             return f_bank
 
-        f_banks = [turn(q, (0, 1)) for q in range(F_BANKS)]
-        for k in range(K):
-            f_k = f_banks[k // K_PER_BANK][:, k % K_PER_BANK, :]
-            if k in SCALAR_K:
-                nc.vector.tensor_scalar_mul(out=f_sbuf[:, k, 0:ROWS], in0=f_k, scalar1=0.5)
-            else:
-                nc.scalar.copy(out=f_sbuf[:, k, 0:ROWS], in_=f_k)
-        nc.vector.tensor_copy(out=f_sbuf[:, :, ROWS:WRAPPED], in_=f_sbuf[:, :, 0:WINDOW])
+        f_banks = {}
+        for q in (5, 6, 7, 4):
+            f_banks[q] = turn(q, (0, 1))
 
-        max_sum = banks.tile([P, ROWS], F32, name="max_sum", tag="bank7")
+        max_sum = banks.tile([P, ROWS], F32, name="max_sum", tag="bank0")
         for b in range(ROW_BLOCKS):
             for k in MAX_K:
                 nc.tensor.matmul(
@@ -213,11 +223,19 @@ def tile_minibatchdiscriminator_kernel(tc, tensor, T, out):
                     start=(k == MAX_K[0]),
                     stop=(k == MAX_K[-1]),
                 )
+        for q in (3, 2, 1, 0):
+            f_banks[q] = turn(q, (0, 1))
+
+        for q in (5, 6, 7, 4):
+            for h in range(K_PER_BANK):
+                k = K_PER_BANK * q + h
+                if k in SCALAR_K:
+                    nc.scalar.mul(f_sbuf[:, k, 0:ROWS], f_banks[q][:, h, :], 0.5)
         nc.vector.tensor_scalar_mul(out=half_sum[:], in0=max_sum[:], scalar1=0.5)
-        for first, last in ((0, ROWS), (ROWS, WRAPPED)):
-            nc.vector.tensor_scalar_mul(
-                out=minus_half_sum[:, first:last], in0=max_sum[:, 0 : last - first], scalar1=-0.5
-            )
+        nc.vector.tensor_scalar_mul(out=minus_half_sum[:, 0:ROWS], in0=max_sum[:], scalar1=-0.5)
+        for k in reversed(MAX_K):
+            f_k = f_banks[k // K_PER_BANK][:, k % K_PER_BANK, :]
+            nc.vector.tensor_copy(out=f_sbuf[:, k, 0:ROWS], in_=f_k)
 
         work = pools.enter_context(tc.tile_pool(name="work", bufs=3))
 
@@ -281,17 +299,6 @@ def tile_minibatchdiscriminator_kernel(tc, tensor, T, out):
 
         def add_up(quad, lone, acc, by_scalar):
             half = banks.tile([P, QUAD, J], F32, name="half", tag="bank%d" % (3 + quad % 2))
-            if quad % WAKE_EVERY == 0:
-                for g in range(WAKE_PASSES):
-                    nc.tensor.matmul_mx(
-                        out=half[:].rearrange("p i j -> p (i j)"),
-                        lhsT=x_codes[:, g, 0:P].bitcast(FP8X4),
-                        lhsT_scale=x_scales[:, g, 0:P],
-                        rhs=t_codes[:, g, 0:BANK].bitcast(FP8X4),
-                        rhs_scale=t_scales[:, g, 0:BANK],
-                        start=(g == 0),
-                        stop=(g == WAKE_PASSES - 1),
-                    )
             for i in reversed(range(QUAD)):
                 summands = [acc[:, i, :]]
                 summands += [by_scalar[:, i, h, :] for h in reversed(range(len(SCALAR_K)))]
@@ -301,7 +308,9 @@ def tile_minibatchdiscriminator_kernel(tc, tensor, T, out):
                         out=half[:, i, :],
                         lhsT=summand,
                         rhs=identity[:],
-                        is_transpose=True,
+                        is_transpose=not (
+                            s == 0 and i == QUAD - 1 and quad % QUADS_PER_ROUND < PLAIN_QUADS
+                        ),
                         start=(s == 0),
                         stop=(s == len(summands) - 1),
                     )
@@ -381,6 +390,14 @@ def tile_minibatchdiscriminator_kernel(tc, tensor, T, out):
             turned = {}
             others = None
             for t in range(QUADS + 4):
+                if t == HALF - 1:
+                    first = LONE_K[0]
+                    nc.vector.tensor_copy(
+                        out=f_sbuf[:, first:K, ROWS:WRAPPED], in_=f_sbuf[:, first:K, 0:WINDOW]
+                    )
+                    nc.vector.tensor_copy(
+                        out=minus_half_sum[:, ROWS:WRAPPED], in_=minus_half_sum[:, 0:WINDOW]
+                    )
                 if t == HALF:
                     f_banks = [turn(q, (1, 0)) for q in range((len(CHAIN_K) + 1) // K_PER_BANK)]
                 if 0 <= t - 2 < QUADS:
@@ -390,13 +407,13 @@ def tile_minibatchdiscriminator_kernel(tc, tensor, T, out):
                 if 0 <= t - 1 < QUADS:
                     halves[t - 1] = add_up(t - 1, *leaves[t - 1])
                 quad = t - 3
+                if quad in (HALF, QUADS):
+                    add_others(others, base_of(quad - 1))
                 if 0 <= quad < QUADS:
                     if quad % HALF == 0:
                         others = open_others(base_of(quad))
                     last = quad % HALF == HALF - 1
                     turned[quad] = turn_back(quad, es[quad], others, last)
-                    if last:
-                        add_others(others, base_of(quad))
                 if 0 <= t - 4 < QUADS:
                     sum_over_later(t - 4, turned[t - 4])
 

@@ -31,10 +31,12 @@ K_PER_BANK = BANK // ROWS
 F_BANKS = K // K_PER_BANK
 WINDOW = P
 WRAPPED = ROWS + WINDOW
-CHAIN_K = range(0, 5)
-LONE_K = range(5, 9)
+CHAIN_K = range(0, 7)
+POOL_K = range(7, 9)
 SCALAR_K = range(9, 16)
 MAX_K = range(0, 9)
+CHAIN_BANKS = 4
+HUGE = 3.0e38
 PLAIN_QUADS = 3
 QUADS_PER_ROUND = 4
 QUAD = BANK // J
@@ -49,6 +51,8 @@ def tile_minibatchdiscriminator_kernel(tc, tensor, T, out):
     with ExitStack() as pools:
         keep = pools.enter_context(tc.tile_pool(name="keep", bufs=1))
         banks = pools.enter_context(tc.psum_pool(name="banks", bufs=1))
+
+        pools.enter_context(tc.manual_schedule())
 
         identity = keep.tile([P, P], F32)
         make_identity(nc, identity[:])
@@ -68,7 +72,6 @@ def tile_minibatchdiscriminator_kernel(tc, tensor, T, out):
 
         f_sbuf = keep.tile([P, K, WRAPPED], F32)
         f_rows = [keep.tile([P, K, J], F32, name="f_rows%d" % b) for b in range(ROW_BLOCKS)]
-        half_sum = keep.tile([P, ROWS], F32)
         minus_half_sum = keep.tile([P, WRAPPED], F32)
         zeros = keep.tile([P, P], F32)
         from_later = keep.tile([P, ROWS], F32)
@@ -209,10 +212,9 @@ def tile_minibatchdiscriminator_kernel(tc, tensor, T, out):
             return f_bank
 
         f_banks = {}
-        for q in (5, 6, 7, 4):
+        for q in (4, 5, 3):
             f_banks[q] = turn(q, (0, 1))
-
-        max_sum = banks.tile([P, ROWS], F32, name="max_sum", tag="bank0")
+        max_sum = banks.tile([P, ROWS], F32, name="max_sum", tag="bank2")
         for b in range(ROW_BLOCKS):
             for k in MAX_K:
                 nc.tensor.matmul(
@@ -223,19 +225,15 @@ def tile_minibatchdiscriminator_kernel(tc, tensor, T, out):
                     start=(k == MAX_K[0]),
                     stop=(k == MAX_K[-1]),
                 )
-        for q in (3, 2, 1, 0):
+        for q in (6, 0, 7, 1, 2):
             f_banks[q] = turn(q, (0, 1))
 
-        for q in (5, 6, 7, 4):
-            for h in range(K_PER_BANK):
-                k = K_PER_BANK * q + h
-                if k in SCALAR_K:
-                    nc.scalar.mul(f_sbuf[:, k, 0:ROWS], f_banks[q][:, h, :], 0.5)
-        nc.vector.tensor_scalar_mul(out=half_sum[:], in0=max_sum[:], scalar1=0.5)
-        nc.vector.tensor_scalar_mul(out=minus_half_sum[:, 0:ROWS], in0=max_sum[:], scalar1=-0.5)
-        for k in reversed(MAX_K):
+        def keep_f(k):
             f_k = f_banks[k // K_PER_BANK][:, k % K_PER_BANK, :]
-            nc.vector.tensor_copy(out=f_sbuf[:, k, 0:ROWS], in_=f_k)
+            if k in SCALAR_K:
+                nc.scalar.mul(f_sbuf[:, k, 0:ROWS], f_k, 0.5)
+            else:
+                nc.vector.tensor_copy(out=f_sbuf[:, k, 0:ROWS], in_=f_k)
 
         work = pools.enter_context(tc.tile_pool(name="work", bufs=3))
 
@@ -248,61 +246,56 @@ def tile_minibatchdiscriminator_kernel(tc, tensor, T, out):
         def window(n):
             return slice(n + 1, n + 1 + WINDOW)
 
-        def lone_maxima(quad):
-            leaves = work.tile([P, QUAD, len(LONE_K), WINDOW], F32, name="lone")
+        def chain_starts(quad, acc):
             for i, n in enumerate(rows_of(quad)):
-                for h, k in enumerate(LONE_K):
-                    if h == 0:
-                        nc.vector.tensor_scalar(
-                            out=leaves[:, i, h, :],
-                            in0=f_sbuf[:, k, window(n)],
-                            scalar1=f_sbuf[:, k, n : n + 1],
-                            scalar2=half_sum[:, n : n + 1],
-                            op0=ALU.max,
-                            op1=ALU.subtract,
-                        )
-                    else:
-                        nc.vector.tensor_scalar_max(
-                            out=leaves[:, i, h, :],
-                            in0=f_sbuf[:, k, window(n)],
-                            scalar1=f_sbuf[:, k, n : n + 1],
-                        )
-            return leaves
+                nc.gpsimd.tensor_scalar(
+                    out=acc[:, i, :],
+                    in0=minus_half_sum[:, window(n)],
+                    scalar1=1.0,
+                    scalar2=minus_half_sum[:, n : n + 1],
+                    op0=ALU.mult,
+                    op1=ALU.add,
+                )
 
-        def chains(quad, f_banks):
-            acc = work.tile([P, QUAD, WINDOW], F32, name="acc")
-            for k in CHAIN_K:
-                for i, n in enumerate(rows_of(quad)):
-                    first = n + 1 - base_of(quad)
-                    nc.vector.scalar_tensor_tensor(
-                        out=acc[:, i, :],
-                        in0=f_banks[k // K_PER_BANK][:, k % K_PER_BANK, first : first + WINDOW],
-                        scalar=f_sbuf[:, k, n : n + 1],
-                        in1=minus_half_sum[:, window(n)] if k == CHAIN_K[0] else acc[:, i, :],
-                        op0=ALU.max,
-                        op1=ALU.add,
-                    )
-            return acc
-
-        def absolute_differences(quad):
-            leaves = work.tile([P, QUAD, len(SCALAR_K), WINDOW], F32, name="scalar_leaves")
+        def chain_link(quad, acc, k, f_banks):
             for i, n in enumerate(rows_of(quad)):
-                for h, k in enumerate(SCALAR_K):
-                    nc.scalar.activation(
-                        out=leaves[:, i, h, :],
-                        in_=f_sbuf[:, k, window(n)],
-                        func=ACT.Abs,
-                        bias=f_sbuf[:, k, n : n + 1],
-                        scale=-1.0,
-                    )
-            return leaves
+                first = n + 1 - base_of(quad)
+                nc.vector.scalar_tensor_tensor(
+                    out=acc[:, i, :],
+                    in0=f_banks[k // K_PER_BANK][:, k % K_PER_BANK, first : first + WINDOW],
+                    scalar=f_sbuf[:, k, n : n + 1],
+                    in1=acc[:, i, :],
+                    op0=ALU.max,
+                    op1=ALU.add,
+                )
 
-        def add_up(quad, lone, acc, by_scalar):
-            half = banks.tile([P, QUAD, J], F32, name="half", tag="bank%d" % (3 + quad % 2))
+        def pool_maxima(quad, leaves, k):
+            for i, n in enumerate(rows_of(quad)):
+                nc.gpsimd.tensor_scalar(
+                    out=leaves[:, i, k - POOL_K[0], :],
+                    in0=f_sbuf[:, k, window(n)],
+                    scalar1=HUGE,
+                    scalar2=f_sbuf[:, k, n : n + 1],
+                    op0=ALU.min,
+                    op1=ALU.max,
+                )
+
+        def absolute_differences(quad, leaves, k):
+            for i, n in enumerate(rows_of(quad)):
+                nc.scalar.activation(
+                    out=leaves[:, i, k - SCALAR_K[0], :],
+                    in_=f_sbuf[:, k, window(n)],
+                    func=ACT.Abs,
+                    bias=f_sbuf[:, k, n : n + 1],
+                    scale=-1.0,
+                )
+
+        def add_up(quad, by_pool, acc, by_scalar):
+            half = banks.tile([P, QUAD, J], F32, name="half", tag="bank%d" % (4 + quad % 2))
             for i in reversed(range(QUAD)):
                 summands = [acc[:, i, :]]
                 summands += [by_scalar[:, i, h, :] for h in reversed(range(len(SCALAR_K)))]
-                summands += [lone[:, i, h, :] for h in reversed(range(len(LONE_K)))]
+                summands += [by_pool[:, i, h, :] for h in reversed(range(len(POOL_K)))]
                 for s, summand in enumerate(summands):
                     nc.tensor.matmul(
                         out=half[:, i, :],
@@ -340,7 +333,7 @@ def tile_minibatchdiscriminator_kernel(tc, tensor, T, out):
             return others
 
         def turn_back(quad, e, others, last):
-            turned = banks.tile([P, QUAD, WINDOW], F32, name="turned", tag="bank%d" % (5 + quad % 2))
+            turned = banks.tile([P, QUAD, WINDOW], F32, name="turned", tag="bank6")
             for i in range(QUAD):
                 nc.tensor.transpose(turned[:, i, :], e[:, i, :], identity[:])
             for i, n in enumerate(rows_of(quad)):
@@ -383,39 +376,62 @@ def tile_minibatchdiscriminator_kernel(tc, tensor, T, out):
 
         QUADS = ROWS // QUAD
         HALF = QUADS // 2
-        with tc.manual_schedule():
-            leaves = {}
-            halves = {}
-            es = {}
-            turned = {}
-            others = None
-            for t in range(QUADS + 4):
-                if t == HALF - 1:
-                    first = LONE_K[0]
-                    nc.vector.tensor_copy(
-                        out=f_sbuf[:, first:K, ROWS:WRAPPED], in_=f_sbuf[:, first:K, 0:WINDOW]
+        leaves = {}
+        halves = {}
+        es = {}
+        turned = {}
+        others = None
+        for t in range(QUADS + 4):
+            if t == HALF - 1:
+                nc.vector.tensor_copy(
+                    out=f_sbuf[:, POOL_K[0] : K, ROWS:WRAPPED],
+                    in_=f_sbuf[:, POOL_K[0] : K, 0:WINDOW],
+                )
+                nc.vector.tensor_copy(
+                    out=minus_half_sum[:, ROWS:WRAPPED], in_=minus_half_sum[:, 0:WINDOW]
+                )
+            if t == HALF:
+                f_banks = [turn(q, (1, 0)) for q in range(CHAIN_BANKS)]
+            if t < QUADS:
+                by_scalar = work.tile([P, QUAD, len(SCALAR_K), WINDOW], F32, name="by_scalar")
+                by_pool = work.tile([P, QUAD, len(POOL_K), WINDOW], F32, name="by_pool")
+                acc = work.tile([P, QUAD, WINDOW], F32, name="acc")
+                leaves[t] = (by_pool, acc, by_scalar)
+                for k in SCALAR_K:
+                    if k == SCALAR_K[len(SCALAR_K) // 2] and t >= 2:
+                        es[t - 2] = exponentials(halves[t - 2])
+                    if t == 0:
+                        keep_f(k)
+                    absolute_differences(t, by_scalar, k)
+                if t == 0:
+                    nc.vector.tensor_scalar_mul(
+                        out=minus_half_sum[:, 0:ROWS], in0=max_sum[:], scalar1=-0.5
                     )
-                    nc.vector.tensor_copy(
-                        out=minus_half_sum[:, ROWS:WRAPPED], in_=minus_half_sum[:, 0:WINDOW]
-                    )
-                if t == HALF:
-                    f_banks = [turn(q, (1, 0)) for q in range((len(CHAIN_K) + 1) // K_PER_BANK)]
-                if 0 <= t - 2 < QUADS:
+                chain_starts(t, acc)
+                for k in POOL_K:
+                    if t == 0:
+                        keep_f(k)
+                    pool_maxima(t, by_pool, k)
+                for k in CHAIN_K:
+                    if t == 0:
+                        keep_f(k)
+                    chain_link(t, acc, k, f_banks)
+                    if k == CHAIN_K[len(CHAIN_K) // 2] and t >= 4:
+                        sum_over_later(t - 4, turned[t - 4])
+            else:
+                if t - 2 < QUADS:
                     es[t - 2] = exponentials(halves[t - 2])
-                if t < QUADS:
-                    leaves[t] = (lone_maxima(t), chains(t, f_banks), absolute_differences(t))
-                if 0 <= t - 1 < QUADS:
-                    halves[t - 1] = add_up(t - 1, *leaves[t - 1])
-                quad = t - 3
-                if quad in (HALF, QUADS):
-                    add_others(others, base_of(quad - 1))
-                if 0 <= quad < QUADS:
-                    if quad % HALF == 0:
-                        others = open_others(base_of(quad))
-                    last = quad % HALF == HALF - 1
-                    turned[quad] = turn_back(quad, es[quad], others, last)
-                if 0 <= t - 4 < QUADS:
-                    sum_over_later(t - 4, turned[t - 4])
+                sum_over_later(t - 4, turned[t - 4])
+            if 0 <= t - 1 < QUADS:
+                halves[t - 1] = add_up(t - 1, *leaves[t - 1])
+            quad = t - 3
+            if quad in (HALF, QUADS):
+                add_others(others, base_of(quad - 1))
+            if 0 <= quad < QUADS:
+                if quad % HALF == 0:
+                    others = open_others(base_of(quad))
+                last = quad % HALF == HALF - 1
+                turned[quad] = turn_back(quad, es[quad], others, last)
 
         nc.vector.tensor_tensor(
             out=diversity[:], in0=from_later[:], in1=diversity[:], op=ALU.add

@@ -246,28 +246,28 @@ def tile_minibatchdiscriminator_kernel(tc, tensor, T, out):
         def window(n):
             return slice(n + 1, n + 1 + WINDOW)
 
-        def chain_starts(quad, acc):
-            for i, n in enumerate(rows_of(quad)):
-                nc.gpsimd.tensor_scalar(
-                    out=acc[:, i, :],
-                    in0=minus_half_sum[:, window(n)],
-                    scalar1=1.0,
-                    scalar2=minus_half_sum[:, n : n + 1],
-                    op0=ALU.mult,
-                    op1=ALU.add,
-                )
-
         def chain_link(quad, acc, k, f_banks):
             for i, n in enumerate(rows_of(quad)):
                 first = n + 1 - base_of(quad)
-                nc.vector.scalar_tensor_tensor(
-                    out=acc[:, i, :],
-                    in0=f_banks[k // K_PER_BANK][:, k % K_PER_BANK, first : first + WINDOW],
-                    scalar=f_sbuf[:, k, n : n + 1],
-                    in1=acc[:, i, :],
-                    op0=ALU.max,
-                    op1=ALU.add,
-                )
+                f_k = f_banks[k // K_PER_BANK][:, k % K_PER_BANK, first : first + WINDOW]
+                if k == CHAIN_K[0]:
+                    nc.vector.tensor_scalar(
+                        out=acc[:, i, :],
+                        in0=f_k,
+                        scalar1=f_sbuf[:, k, n : n + 1],
+                        scalar2=minus_half_sum[:, n : n + 1],
+                        op0=ALU.max,
+                        op1=ALU.add,
+                    )
+                else:
+                    nc.vector.scalar_tensor_tensor(
+                        out=acc[:, i, :],
+                        in0=f_k,
+                        scalar=f_sbuf[:, k, n : n + 1],
+                        in1=acc[:, i, :],
+                        op0=ALU.max,
+                        op1=ALU.add,
+                    )
 
         def pool_maxima(quad, leaves, k):
             for i, n in enumerate(rows_of(quad)):
@@ -292,8 +292,9 @@ def tile_minibatchdiscriminator_kernel(tc, tensor, T, out):
 
         def add_up(quad, by_pool, acc, by_scalar):
             half = banks.tile([P, QUAD, J], F32, name="half", tag="bank%d" % (4 + quad % 2))
-            for i in reversed(range(QUAD)):
-                summands = [acc[:, i, :]]
+            plain = quad % QUADS_PER_ROUND < PLAIN_QUADS
+            for i, n in reversed(list(enumerate(rows_of(quad)))):
+                summands = [acc[:, i, :], minus_half_sum[:, window(n)]]
                 summands += [by_scalar[:, i, h, :] for h in reversed(range(len(SCALAR_K)))]
                 summands += [by_pool[:, i, h, :] for h in reversed(range(len(POOL_K)))]
                 for s, summand in enumerate(summands):
@@ -301,9 +302,7 @@ def tile_minibatchdiscriminator_kernel(tc, tensor, T, out):
                         out=half[:, i, :],
                         lhsT=summand,
                         rhs=identity[:],
-                        is_transpose=not (
-                            s == 0 and i == QUAD - 1 and quad % QUADS_PER_ROUND < PLAIN_QUADS
-                        ),
+                        is_transpose=not (plain and s == 0 and i == QUAD - 1),
                         start=(s == 0),
                         stop=(s == len(summands) - 1),
                     )
@@ -379,9 +378,8 @@ def tile_minibatchdiscriminator_kernel(tc, tensor, T, out):
         leaves = {}
         halves = {}
         es = {}
-        turned = {}
         others = None
-        for t in range(QUADS + 4):
+        for t in range(QUADS + 3):
             if t == HALF - 1:
                 nc.vector.tensor_copy(
                     out=f_sbuf[:, POOL_K[0] : K, ROWS:WRAPPED],
@@ -392,6 +390,13 @@ def tile_minibatchdiscriminator_kernel(tc, tensor, T, out):
                 )
             if t == HALF:
                 f_banks = [turn(q, (1, 0)) for q in range(CHAIN_BANKS)]
+            back = t - 3
+            if back == HALF:
+                add_others(others, base_of(back - 1))
+            if back >= 0:
+                if back % HALF == 0:
+                    others = open_others(base_of(back))
+                turned = turn_back(back, es[back], others, back % HALF == HALF - 1)
             if t < QUADS:
                 by_scalar = work.tile([P, QUAD, len(SCALAR_K), WINDOW], F32, name="by_scalar")
                 by_pool = work.tile([P, QUAD, len(POOL_K), WINDOW], F32, name="by_pool")
@@ -407,7 +412,6 @@ def tile_minibatchdiscriminator_kernel(tc, tensor, T, out):
                     nc.vector.tensor_scalar_mul(
                         out=minus_half_sum[:, 0:ROWS], in0=max_sum[:], scalar1=-0.5
                     )
-                chain_starts(t, acc)
                 for k in POOL_K:
                     if t == 0:
                         keep_f(k)
@@ -416,22 +420,15 @@ def tile_minibatchdiscriminator_kernel(tc, tensor, T, out):
                     if t == 0:
                         keep_f(k)
                     chain_link(t, acc, k, f_banks)
-                    if k == CHAIN_K[len(CHAIN_K) // 2] and t >= 4:
-                        sum_over_later(t - 4, turned[t - 4])
+                    if k == CHAIN_K[len(CHAIN_K) // 2] and back >= 0:
+                        sum_over_later(back, turned)
             else:
                 if t - 2 < QUADS:
                     es[t - 2] = exponentials(halves[t - 2])
-                sum_over_later(t - 4, turned[t - 4])
-            if 0 <= t - 1 < QUADS:
+                sum_over_later(back, turned)
+            if 1 <= t <= QUADS:
                 halves[t - 1] = add_up(t - 1, *leaves[t - 1])
-            quad = t - 3
-            if quad in (HALF, QUADS):
-                add_others(others, base_of(quad - 1))
-            if 0 <= quad < QUADS:
-                if quad % HALF == 0:
-                    others = open_others(base_of(quad))
-                last = quad % HALF == HALF - 1
-                turned[quad] = turn_back(quad, es[quad], others, last)
+        add_others(others, base_of(QUADS - 1))
 
         nc.vector.tensor_tensor(
             out=diversity[:], in0=from_later[:], in1=diversity[:], op=ALU.add

@@ -31,10 +31,14 @@ K_PER_BANK = BANK // ROWS
 F_BANKS = K // K_PER_BANK
 WINDOW = P
 WRAPPED = ROWS + WINDOW
-CHAIN_K = range(0, 7)
-POOL_K = range(7, 9)
-SCALAR_K = range(9, 16)
-MAX_K = range(0, 9)
+SHARES = (
+    (range(0, 7), range(7, 9), range(9, 16)),
+    (range(0, 8), range(8, 10), range(10, 16)),
+    (range(0, 7), range(7, 9), range(9, 16)),
+    (range(0, 7), range(7, 10), range(10, 16)),
+)
+SHARED_K = 9
+F_SLOTS = K + 1
 CHAIN_BANKS = 4
 HUGE = 3.0e38
 PLAIN_QUADS = 3
@@ -70,9 +74,9 @@ def tile_minibatchdiscriminator_kernel(tc, tensor, T, out):
             )
             x_halves.append(half_of)
 
-        f_sbuf = keep.tile([P, K, WRAPPED], F32)
+        f_sbuf = keep.tile([P, F_SLOTS, WRAPPED], F32)
         f_rows = [keep.tile([P, K, J], F32, name="f_rows%d" % b) for b in range(ROW_BLOCKS)]
-        minus_half_sum = keep.tile([P, WRAPPED], F32)
+        minus_half_sum = keep.tile([P, 2, WRAPPED], F32)
         zeros = keep.tile([P, P], F32)
         from_later = keep.tile([P, ROWS], F32)
         diversity = keep.tile([P, ROWS], F32)
@@ -212,28 +216,29 @@ def tile_minibatchdiscriminator_kernel(tc, tensor, T, out):
             return f_bank
 
         f_banks = {}
-        for q in (4, 5, 3):
+        for q in (4, 5, 3, 0, 6, 1, 2):
             f_banks[q] = turn(q, (0, 1))
-        max_sum = banks.tile([P, ROWS], F32, name="max_sum", tag="bank2")
+        max_sum = banks.tile([P, ROWS], F32, name="max_sum", tag="bank7")
         for b in range(ROW_BLOCKS):
-            for k in MAX_K:
+            for k in range(SHARED_K):
                 nc.tensor.matmul(
                     out=max_sum[:, b * P : (b + 1) * P],
                     lhsT=f_rows[b][:, k, :],
                     rhs=identity[:],
                     is_transpose=True,
-                    start=(k == MAX_K[0]),
-                    stop=(k == MAX_K[-1]),
+                    start=(k == 0),
+                    stop=(k == SHARED_K - 1),
                 )
-        for q in (6, 0, 7, 1, 2):
-            f_banks[q] = turn(q, (0, 1))
+        f_banks[7] = turn(7, (0, 1))
+
+        def in_psum(k):
+            return f_banks[k // K_PER_BANK][:, k % K_PER_BANK, :]
 
         def keep_f(k):
-            f_k = f_banks[k // K_PER_BANK][:, k % K_PER_BANK, :]
-            if k in SCALAR_K:
-                nc.scalar.mul(f_sbuf[:, k, 0:ROWS], f_k, 0.5)
+            if k < SHARED_K:
+                nc.vector.tensor_copy(out=f_sbuf[:, k, 0:ROWS], in_=in_psum(k))
             else:
-                nc.vector.tensor_copy(out=f_sbuf[:, k, 0:ROWS], in_=f_k)
+                nc.scalar.mul(f_sbuf[:, k, 0:ROWS], in_psum(k), 0.5)
 
         work = pools.enter_context(tc.tile_pool(name="work", bufs=3))
 
@@ -246,16 +251,22 @@ def tile_minibatchdiscriminator_kernel(tc, tensor, T, out):
         def window(n):
             return slice(n + 1, n + 1 + WINDOW)
 
+        def share_of(quad):
+            return SHARES[quad % len(SHARES)]
+
+        def corrections(quad):
+            return minus_half_sum[:, 1 if share_of(quad)[1][-1] == SHARED_K else 0, :]
+
         def chain_link(quad, acc, k, f_banks):
             for i, n in enumerate(rows_of(quad)):
                 first = n + 1 - base_of(quad)
                 f_k = f_banks[k // K_PER_BANK][:, k % K_PER_BANK, first : first + WINDOW]
-                if k == CHAIN_K[0]:
+                if k == 0:
                     nc.vector.tensor_scalar(
                         out=acc[:, i, :],
                         in0=f_k,
                         scalar1=f_sbuf[:, k, n : n + 1],
-                        scalar2=minus_half_sum[:, n : n + 1],
+                        scalar2=corrections(quad)[:, n : n + 1],
                         op0=ALU.max,
                         op1=ALU.add,
                     )
@@ -270,12 +281,13 @@ def tile_minibatchdiscriminator_kernel(tc, tensor, T, out):
                     )
 
         def pool_maxima(quad, leaves, k):
+            slot = K if k == SHARED_K else k
             for i, n in enumerate(rows_of(quad)):
                 nc.gpsimd.tensor_scalar(
-                    out=leaves[:, i, k - POOL_K[0], :],
-                    in0=f_sbuf[:, k, window(n)],
+                    out=leaves[:, i, k - share_of(quad)[1][0], :],
+                    in0=f_sbuf[:, slot, window(n)],
                     scalar1=HUGE,
-                    scalar2=f_sbuf[:, k, n : n + 1],
+                    scalar2=f_sbuf[:, slot, n : n + 1],
                     op0=ALU.min,
                     op1=ALU.max,
                 )
@@ -283,7 +295,7 @@ def tile_minibatchdiscriminator_kernel(tc, tensor, T, out):
         def absolute_differences(quad, leaves, k):
             for i, n in enumerate(rows_of(quad)):
                 nc.scalar.activation(
-                    out=leaves[:, i, k - SCALAR_K[0], :],
+                    out=leaves[:, i, k - share_of(quad)[2][0], :],
                     in_=f_sbuf[:, k, window(n)],
                     func=ACT.Abs,
                     bias=f_sbuf[:, k, n : n + 1],
@@ -294,9 +306,9 @@ def tile_minibatchdiscriminator_kernel(tc, tensor, T, out):
             half = banks.tile([P, QUAD, J], F32, name="half", tag="bank%d" % (4 + quad % 2))
             plain = quad % QUADS_PER_ROUND < PLAIN_QUADS
             for i, n in reversed(list(enumerate(rows_of(quad)))):
-                summands = [acc[:, i, :], minus_half_sum[:, window(n)]]
-                summands += [by_scalar[:, i, h, :] for h in reversed(range(len(SCALAR_K)))]
-                summands += [by_pool[:, i, h, :] for h in reversed(range(len(POOL_K)))]
+                summands = [acc[:, i, :], corrections(quad)[:, window(n)]]
+                for part in (by_scalar, by_pool):
+                    summands += [part[:, i, h, :] for h in reversed(range(part.shape[2]))]
                 for s, summand in enumerate(summands):
                     nc.tensor.matmul(
                         out=half[:, i, :],
@@ -381,13 +393,8 @@ def tile_minibatchdiscriminator_kernel(tc, tensor, T, out):
         others = None
         for t in range(QUADS + 3):
             if t == HALF - 1:
-                nc.vector.tensor_copy(
-                    out=f_sbuf[:, POOL_K[0] : K, ROWS:WRAPPED],
-                    in_=f_sbuf[:, POOL_K[0] : K, 0:WINDOW],
-                )
-                nc.vector.tensor_copy(
-                    out=minus_half_sum[:, ROWS:WRAPPED], in_=minus_half_sum[:, 0:WINDOW]
-                )
+                for part in (f_sbuf[:, SHARES[0][1][0] : F_SLOTS, :], minus_half_sum[:]):
+                    nc.vector.tensor_copy(out=part[:, :, ROWS:WRAPPED], in_=part[:, :, 0:WINDOW])
             if t == HALF:
                 f_banks = [turn(q, (1, 0)) for q in range(CHAIN_BANKS)]
             back = t - 3
@@ -398,30 +405,39 @@ def tile_minibatchdiscriminator_kernel(tc, tensor, T, out):
                     others = open_others(base_of(back))
                 turned = turn_back(back, es[back], others, back % HALF == HALF - 1)
             if t < QUADS:
-                by_scalar = work.tile([P, QUAD, len(SCALAR_K), WINDOW], F32, name="by_scalar")
-                by_pool = work.tile([P, QUAD, len(POOL_K), WINDOW], F32, name="by_pool")
+                chain_ks, pool_ks, scalar_ks = share_of(t)
+                by_scalar = work.tile([P, QUAD, len(scalar_ks), WINDOW], F32, name="by_scalar")
+                by_pool = work.tile([P, QUAD, len(pool_ks), WINDOW], F32, name="by_pool")
                 acc = work.tile([P, QUAD, WINDOW], F32, name="acc")
                 leaves[t] = (by_pool, acc, by_scalar)
-                for k in SCALAR_K:
-                    if k == SCALAR_K[len(SCALAR_K) // 2] and t >= 2:
+                for k in scalar_ks:
+                    if k == scalar_ks[len(scalar_ks) // 2] and t >= 2:
                         es[t - 2] = exponentials(halves[t - 2])
                     if t == 0:
                         keep_f(k)
                     absolute_differences(t, by_scalar, k)
                 if t == 0:
+                    for k in (8, 7, 6, 0, 1, 2, 3, 4, 5):
+                        keep_f(k)
                     nc.vector.tensor_scalar_mul(
-                        out=minus_half_sum[:, 0:ROWS], in0=max_sum[:], scalar1=-0.5
+                        out=minus_half_sum[:, 0, 0:ROWS], in0=max_sum[:], scalar1=-0.5
                     )
-                for k in POOL_K:
-                    if t == 0:
-                        keep_f(k)
+                for k in pool_ks:
                     pool_maxima(t, by_pool, k)
-                for k in CHAIN_K:
-                    if t == 0:
-                        keep_f(k)
+                for k in chain_ks:
                     chain_link(t, acc, k, f_banks)
-                    if k == CHAIN_K[len(CHAIN_K) // 2] and back >= 0:
+                    if k == chain_ks[len(chain_ks) // 2] and back >= 0:
                         sum_over_later(back, turned)
+                if t == 0:
+                    nc.vector.tensor_copy(out=f_sbuf[:, K, 0:ROWS], in_=in_psum(SHARED_K))
+                    nc.vector.scalar_tensor_tensor(
+                        out=minus_half_sum[:, 1, 0:ROWS],
+                        in0=in_psum(SHARED_K),
+                        scalar=-0.5,
+                        in1=minus_half_sum[:, 0, 0:ROWS],
+                        op0=ALU.mult,
+                        op1=ALU.add,
+                    )
             else:
                 if t - 2 < QUADS:
                     es[t - 2] = exponentials(halves[t - 2])

@@ -31,11 +31,18 @@ K_PER_BANK = BANK // ROWS
 F_BANKS = K // K_PER_BANK
 WINDOW = P
 WRAPPED = ROWS + WINDOW
+COMMON = (range(0, 7), range(7, 9), range(9, 16))
+LIGHT_FOR_SCALAR = (range(0, 7), range(7, 10), range(10, 16))
+LIGHT_FOR_VECTOR = (range(0, 6), range(6, 9), range(9, 16))
 SHARES = (
-    (range(0, 7), range(7, 9), range(9, 16)),
-    (range(0, 8), range(8, 10), range(10, 16)),
-    (range(0, 7), range(7, 9), range(9, 16)),
-    (range(0, 7), range(7, 10), range(10, 16)),
+    COMMON,
+    LIGHT_FOR_SCALAR,
+    COMMON,
+    LIGHT_FOR_VECTOR,
+    COMMON,
+    LIGHT_FOR_SCALAR,
+    COMMON,
+    COMMON,
 )
 SHARED_K = 9
 F_SLOTS = K + 1
@@ -80,11 +87,13 @@ def tile_minibatchdiscriminator_kernel(tc, tensor, T, out):
         zeros = keep.tile([P, P], F32)
         from_later = keep.tile([P, ROWS], F32)
         diversity = keep.tile([P, ROWS], F32)
+        late_others = keep.tile([P, 1 + 2 * ROWS], F32)
         d_rows = keep.tile([P, ROW_BLOCKS, J], F32)
 
         nc.vector.memset(zeros[:], 0.0)
         nc.scalar.activation(out=d_rows[:, 0, 0:1], in_=zeros[:, 0:1], func=ACT.Exp)
         nc.vector.memset(diversity[:], 1.0)
+        nc.vector.memset(late_others[:, 0:1], 0.0)
 
         with tc.tile_pool(name="stage", bufs=1) as stage:
             x_codes = stage.tile([P, PASSES, ROWS], U32, align_bytes=64)
@@ -370,20 +379,14 @@ def tile_minibatchdiscriminator_kernel(tc, tensor, T, out):
                 op=ALU.add,
             )
 
-        def add_others(others, base):
-            for shift, first in ((1, 0), (0, ROWS)):
-                width = ROWS - shift
-                before_wrap = min(width, ROWS - base - shift)
-                pieces = [(base + shift, first, before_wrap)]
-                if before_wrap < width:
-                    pieces.append((0, first + before_wrap, width - before_wrap))
-                for row, column, count in pieces:
-                    nc.vector.tensor_tensor(
-                        out=diversity[:, row : row + count],
-                        in0=others[:, column : column + count],
-                        in1=diversity[:, row : row + count],
-                        op=ALU.add,
-                    )
+        def add_first_others(others):
+            for row, first in ((1, 0), (0, ROWS)):
+                nc.vector.tensor_tensor(
+                    out=diversity[:, row:ROWS],
+                    in0=others[:, first : first + ROWS - row],
+                    in1=diversity[:, row:ROWS],
+                    op=ALU.add,
+                )
 
         QUADS = ROWS // QUAD
         HALF = QUADS // 2
@@ -393,13 +396,14 @@ def tile_minibatchdiscriminator_kernel(tc, tensor, T, out):
         others = None
         for t in range(QUADS + 3):
             if t == HALF - 1:
-                for part in (f_sbuf[:, SHARES[0][1][0] : F_SLOTS, :], minus_half_sum[:]):
+                first = min(share[1][0] for share in SHARES)
+                for part in (f_sbuf[:, first:F_SLOTS, :], minus_half_sum[:]):
                     nc.vector.tensor_copy(out=part[:, :, ROWS:WRAPPED], in_=part[:, :, 0:WINDOW])
             if t == HALF:
                 f_banks = [turn(q, (1, 0)) for q in range(CHAIN_BANKS)]
             back = t - 3
             if back == HALF:
-                add_others(others, base_of(back - 1))
+                add_first_others(others)
             if back >= 0:
                 if back % HALF == 0:
                     others = open_others(base_of(back))
@@ -444,14 +448,27 @@ def tile_minibatchdiscriminator_kernel(tc, tensor, T, out):
                 sum_over_later(back, turned)
             if 1 <= t <= QUADS:
                 halves[t - 1] = add_up(t - 1, *leaves[t - 1])
-        add_others(others, base_of(QUADS - 1))
 
-        nc.vector.tensor_tensor(
-            out=diversity[:], in0=from_later[:], in1=diversity[:], op=ALU.add
-        )
+        nc.scalar.copy(out=late_others[:, 1:], in_=others[:])
         d_t = banks.tile([P, ROW_BLOCKS, J], F32, name="d_t", tag="bank0")
         for b in range(ROW_BLOCKS):
-            nc.tensor.transpose(d_t[:, b, :], diversity[:, b * P : (b + 1) * P], identity[:])
+            rows = slice(b * P, (b + 1) * P)
+            late = (b + 1) % ROW_BLOCKS * P
+            summands = (
+                diversity[:, rows],
+                late_others[:, late : late + P],
+                late_others[:, ROWS + 1 + late : ROWS + 1 + late + P],
+                from_later[:, rows],
+            )
+            for s, summand in enumerate(summands):
+                nc.tensor.matmul(
+                    out=d_t[:, b, :],
+                    lhsT=summand,
+                    rhs=identity[:],
+                    is_transpose=True,
+                    start=(s == 0),
+                    stop=(s == len(summands) - 1),
+                )
         nc.vector.tensor_copy(out=d_rows[:], in_=d_t[:])
         nc.sync.dma_start(
             out=out[:, IN_F : IN_F + J].rearrange("(b p) j -> p b j", p=P), in_=d_rows[:]

from contextlib import ExitStack

import concourse.mybir as mybir
from concourse.masks import make_identity

F32 = mybir.dt.float32
BF16 = mybir.dt.bfloat16
U32 = mybir.dt.uint32
U8 = mybir.dt.uint8
FP8X4 = mybir.dt.float8_e4m3fn_x4
ALU = mybir.AluOpType
ACT = mybir.ActivationFunctionType
AXIS = mybir.AxisListType

P = 128
ROWS = 256
ROW_BLOCKS = ROWS // P
IN_F = 2048
J = 128
K = 16
COLS = J * K
PACK = 4
K_PASS = P * PACK
PASSES = IN_F // K_PASS
BANK = 512
COL_BLOCKS = COLS // BANK
SIDES = 2
SIDE = COLS // SIDES
J_PER_BLOCK = BANK // K
K_PER_BANK = BANK // ROWS
F_BANKS = K // K_PER_BANK
WINDOW = P
WRAPPED = ROWS + WINDOW
COMMON = (range(0, 7), range(7, 9), range(9, 16))
LIGHT_FOR_SCALAR = (range(0, 7), range(7, 10), range(10, 16))
LIGHT_FOR_VECTOR = (range(0, 6), range(6, 9), range(9, 16))
SHARES = (
    COMMON,
    LIGHT_FOR_SCALAR,
    COMMON,
    LIGHT_FOR_VECTOR,
    COMMON,
    LIGHT_FOR_SCALAR,
    COMMON,
    COMMON,
)
SHARED_K = 9
F_SLOTS = K + 1
CHAIN_BANKS = 4
HUGE = 3.0e38
PLAIN_QUADS = 3
QUADS_PER_ROUND = 4
QUAD = BANK // J

FLOPS = 2 * ROWS * IN_F * COLS


def tile_minibatchdiscriminator_kernel(tc, tensor, T, out):
    nc = tc.nc
    weights = T.rearrange("i j k -> i (j k)")

    with ExitStack() as pools:
        keep = pools.enter_context(tc.tile_pool(name="keep", bufs=1))
        banks = pools.enter_context(tc.psum_pool(name="banks", bufs=1))

        pools.enter_context(tc.manual_schedule())

        identity = keep.tile([P, P], F32)
        make_identity(nc, identity[:])

        x_rows = keep.tile([P, ROW_BLOCKS * IN_F], BF16)
        x_f32 = keep.tile([P, ROW_BLOCKS * IN_F], F32)
        x_halves = []
        for columns in (slice(0, IN_F // 2), slice(IN_F // 2, IN_F)):
            half_of = [
                tile[:].rearrange("p (b i) -> p b i", b=ROW_BLOCKS)[:, :, columns]
                for tile in (x_rows, x_f32)
            ]
            nc.sync.dma_start(
                out=half_of[0], in_=tensor.rearrange("(b p) i -> p b i", p=P)[:, :, columns]
            )
            x_halves.append(half_of)

        f_sbuf = keep.tile([P, F_SLOTS, WRAPPED], F32)
        f_rows = [keep.tile([P, K, J], F32, name="f_rows%d" % b) for b in range(ROW_BLOCKS)]
        minus_half_sum = keep.tile([P, 2, WRAPPED], F32)
        zeros = keep.tile([P, P], F32)
        from_later = keep.tile([P, ROWS], F32)
        diversity = keep.tile([P, ROWS], F32)
        late_others = keep.tile([P, 1 + 2 * ROWS], F32)
        d_rows = keep.tile([P, ROW_BLOCKS, J], F32)

        nc.vector.memset(zeros[:], 0.0)
        nc.scalar.activation(out=d_rows[:, 0, 0:1], in_=zeros[:, 0:1], func=ACT.Exp)
        nc.vector.memset(diversity[:], 1.0)
        nc.vector.memset(late_others[:, 0:1], 0.0)

        with tc.tile_pool(name="stage", bufs=1) as stage:
            x_codes = stage.tile([P, PASSES, ROWS], U32, align_bytes=64)
            x_scales = stage.tile([P, PASSES, ROWS], U8, align_bytes=64)
            t_codes = stage.tile([P, PASSES, COLS], U32, align_bytes=64)
            t_scales = stage.tile([P, PASSES, COLS], U8, align_bytes=64)
            t_raw = {}
            for side in range(SIDES):
                columns = slice(side * SIDE, (side + 1) * SIDE)
                for g in range(PASSES):
                    raw = stage.tile([P, PACK, SIDE], BF16, name="t_raw%d_%d" % (g, side))
                    rows = weights[K_PASS * g : K_PASS * (g + 1), :]
                    nc.sync.dma_start(
                        out=raw[:], in_=rows.rearrange("(p t) c -> p t c", t=PACK)[:, :, columns]
                    )
                    t_raw[g, side] = raw

            for source, copied in x_halves:
                nc.gpsimd.tensor_scalar(
                    out=copied, in0=source, scalar1=1.0, scalar2=1.0, op0=ALU.mult, op1=ALU.mult
                )
            nc.sync.dma_start(
                out=out[:, 0:IN_F].rearrange("(b p) i -> p b i", p=P),
                in_=x_f32[:].rearrange("p (b i) -> p b i", b=ROW_BLOCKS),
            )

            x_words = x_rows[:].bitcast(F32)
            words_per_row = IN_F // 2
            x_grouped = stage.tile([P, PASSES * ROWS * PACK], BF16, align_bytes=64)
            x_grouped_words = x_grouped[:].bitcast(F32).rearrange(
                "p (g n u) -> p g n u", g=PASSES, u=2
            )
            for g in range(PASSES):
                x_t = banks.tile([P, 2, ROWS], F32, name="x_t%d" % g, tag="bank%d" % g)
                for u in range(2):
                    for b in range(ROW_BLOCKS):
                        first = words_per_row * b + 2 * P * g
                        nc.tensor.transpose(
                            x_t[:, u, b * P : (b + 1) * P],
                            x_words[:, first + u : first + 2 * P : 2],
                            identity[:],
                        )
                nc.scalar.copy(out=x_grouped_words[:, g], in_=x_t[:].rearrange("p u n -> p n u"))

            feats = [
                [
                    banks.tile(
                        [P, BANK],
                        F32,
                        name="feats%d_%d" % (b, c),
                        tag="bank%d" % (COL_BLOCKS * b + c),
                    )
                    for c in range(COL_BLOCKS)
                ]
                for b in range(ROW_BLOCKS)
            ]

            def regroup(g, c):
                grouped = stage.tile(
                    [P, BANK, PACK], BF16, name="t_grouped", bufs=8, align_bytes=64
                )
                copy = nc.vector.tensor_copy if c % 2 == 0 else nc.scalar.copy
                raw = t_raw[g, c * BANK // SIDE]
                first = c * BANK % SIDE
                copy(
                    out=grouped[:].rearrange("p (c i) t -> p c t i", i=4),
                    in_=raw[:, :, first : first + BANK].rearrange("p t (c i) -> p c t i", i=4),
                )
                return grouped

            def quantise_and_multiply(grouped, g, c):
                cols = slice(c * BANK, (c + 1) * BANK)
                nc.vector.quantize_mx(
                    out=t_codes[:, g, cols].bitcast(FP8X4),
                    scales=t_scales[:, g, cols],
                    in_=grouped[:].rearrange("p c t -> p (c t)"),
                )
                for b in range(ROW_BLOCKS):
                    rows = slice(b * P, (b + 1) * P)
                    nc.tensor.matmul_mx(
                        out=feats[b][c][:],
                        lhsT=x_codes[:, g, rows].bitcast(FP8X4),
                        lhsT_scale=x_scales[:, g, rows],
                        rhs=t_codes[:, g, cols].bitcast(FP8X4),
                        rhs_scale=t_scales[:, g, cols],
                        start=(g == 0),
                        stop=(g == PASSES - 1),
                    )

            def sort_by_k(c):
                for b in range(ROW_BLOCKS):
                    copy = nc.vector.tensor_copy if b == 0 else nc.scalar.copy
                    copy(
                        out=f_rows[b][:, :, c * J_PER_BLOCK : (c + 1) * J_PER_BLOCK],
                        in_=feats[b][c][:].rearrange("p (j k) -> p k j", k=K),
                    )

            waiting = None
            for side in range(SIDES):
                for g in range(PASSES):
                    for c in range(side * SIDE // BANK, (side + 1) * SIDE // BANK):
                        grouped = regroup(g, c)
                        if waiting is None:
                            nc.vector.quantize_mx(
                                out=x_codes[:].rearrange("p g n -> p (g n)").bitcast(FP8X4),
                                scales=x_scales[:].rearrange("p g n -> p (g n)"),
                                in_=x_grouped[:],
                            )
                        else:
                            quantise_and_multiply(*waiting)
                        waiting = (grouped, g, c)
                    if side == 1 and g < 2:
                        sort_by_k(g)
            quantise_and_multiply(*waiting)
            sort_by_k(2)
            sort_by_k(3)

        def turn(q, order):
            f_bank = banks.tile(
                [P, K_PER_BANK, ROWS], F32, name="f_bank%d_%d" % (q, order[0]), tag="bank%d" % q
            )
            for h in range(K_PER_BANK):
                for place, b in enumerate(order):
                    nc.tensor.transpose(
                        f_bank[:, h, place * P : (place + 1) * P],
                        f_rows[b][:, K_PER_BANK * q + h, :],
                        identity[:],
                    )
            return f_bank

        f_banks = {}
        for q in (4, 5, 3, 0, 6, 1, 2):
            f_banks[q] = turn(q, (0, 1))
        max_sum = banks.tile([P, ROWS], F32, name="max_sum", tag="bank7")
        for b in range(ROW_BLOCKS):
            for k in range(SHARED_K):
                nc.tensor.matmul(
                    out=max_sum[:, b * P : (b + 1) * P],
                    lhsT=f_rows[b][:, k, :],
                    rhs=identity[:],
                    is_transpose=True,
                    start=(k == 0),
                    stop=(k == SHARED_K - 1),
                )
        f_banks[7] = turn(7, (0, 1))

        def in_psum(k):
            return f_banks[k // K_PER_BANK][:, k % K_PER_BANK, :]

        def keep_f(k):
            if k < SHARED_K:
                nc.vector.tensor_copy(out=f_sbuf[:, k, 0:ROWS], in_=in_psum(k))
            else:
                nc.scalar.mul(f_sbuf[:, k, 0:ROWS], in_psum(k), 0.5)

        work = pools.enter_context(tc.tile_pool(name="work", bufs=3))

        def rows_of(quad):
            return range(QUAD * quad, QUAD * (quad + 1))

        def base_of(quad):
            return rows_of(quad)[0] // P * P

        def window(n):
            return slice(n + 1, n + 1 + WINDOW)

        def share_of(quad):
            return SHARES[quad % len(SHARES)]

        def corrections(quad):
            return minus_half_sum[:, 1 if share_of(quad)[1][-1] == SHARED_K else 0, :]

        def chain_link(quad, acc, k, f_banks):
            for i, n in enumerate(rows_of(quad)):
                first = n + 1 - base_of(quad)
                f_k = f_banks[k // K_PER_BANK][:, k % K_PER_BANK, first : first + WINDOW]
                if k == 0:
                    nc.vector.tensor_scalar(
                        out=acc[:, i, :],
                        in0=f_k,
                        scalar1=f_sbuf[:, k, n : n + 1],
                        scalar2=corrections(quad)[:, n : n + 1],
                        op0=ALU.max,
                        op1=ALU.add,
                    )
                else:
                    nc.vector.scalar_tensor_tensor(
                        out=acc[:, i, :],
                        in0=f_k,
                        scalar=f_sbuf[:, k, n : n + 1],
                        in1=acc[:, i, :],
                        op0=ALU.max,
                        op1=ALU.add,
                    )

        def pool_maxima(quad, leaves, k):
            slot = K if k == SHARED_K else k
            for i, n in enumerate(rows_of(quad)):
                nc.gpsimd.tensor_scalar(
                    out=leaves[:, i, k - share_of(quad)[1][0], :],
                    in0=f_sbuf[:, slot, window(n)],
                    scalar1=HUGE,
                    scalar2=f_sbuf[:, slot, n : n + 1],
                    op0=ALU.min,
                    op1=ALU.max,
                )

        def absolute_differences(quad, leaves, k):
            for i, n in enumerate(rows_of(quad)):
                nc.scalar.activation(
                    out=leaves[:, i, k - share_of(quad)[2][0], :],
                    in_=f_sbuf[:, k, window(n)],
                    func=ACT.Abs,
                    bias=f_sbuf[:, k, n : n + 1],
                    scale=-1.0,
                )

        def add_up(quad, by_pool, acc, by_scalar):
            half = banks.tile([P, QUAD, J], F32, name="half", tag="bank%d" % (4 + quad % 2))
            plain = quad % QUADS_PER_ROUND < PLAIN_QUADS
            for i, n in reversed(list(enumerate(rows_of(quad)))):
                summands = [acc[:, i, :], corrections(quad)[:, window(n)]]
                for part in (by_scalar, by_pool):
                    summands += [part[:, i, h, :] for h in reversed(range(part.shape[2]))]
                for s, summand in enumerate(summands):
                    nc.tensor.matmul(
                        out=half[:, i, :],
                        lhsT=summand,
                        rhs=identity[:],
                        is_transpose=not (plain and s == 0 and i == QUAD - 1),
                        start=(s == 0),
                        stop=(s == len(summands) - 1),
                    )
            return half

        def exponentials(half):
            e = work.tile([P, QUAD, J], F32, name="e")
            nc.scalar.activation(
                out=e[:].rearrange("p i j -> p (i j)"),
                in_=half[:].rearrange("p i j -> p (i j)"),
                func=ACT.Exp,
                scale=-2.0,
            )
            return e

        def open_others(base):
            others = banks.tile([P, 2 * ROWS], F32, name="others%d" % base, tag="bank7")
            for piece in range(2 * ROWS // P):
                nc.tensor.matmul(
                    out=others[:, piece * P : (piece + 1) * P],
                    lhsT=zeros[:],
                    rhs=identity[:],
                    is_transpose=True,
                    start=(piece == 0),
                    stop=False,
                )
            return others

        def turn_back(quad, e, others, last):
            turned = banks.tile([P, QUAD, WINDOW], F32, name="turned", tag="bank6")
            for i in range(QUAD):
                nc.tensor.transpose(turned[:, i, :], e[:, i, :], identity[:])
            for i, n in enumerate(rows_of(quad)):
                place = n - base_of(quad)
                if place % 2 == 1:
                    place += ROWS + 1
                nc.tensor.matmul(
                    out=others[:, place : place + WINDOW],
                    lhsT=e[:, i, :],
                    rhs=identity[:],
                    is_transpose=True,
                    start=False,
                    stop=(last and i == QUAD - 1),
                )
            return turned

        def sum_over_later(quad, turned):
            first = QUAD * quad
            nc.vector.tensor_reduce(
                out=from_later[:, first : first + QUAD],
                in_=turned[:, :, 0 : WINDOW - 1],
                axis=AXIS.X,
                op=ALU.add,
            )

        def add_first_others(others):
            for row, first in ((1, 0), (0, ROWS)):
                nc.vector.tensor_tensor(
                    out=diversity[:, row:ROWS],
                    in0=others[:, first : first + ROWS - row],
                    in1=diversity[:, row:ROWS],
                    op=ALU.add,
                )

        QUADS = ROWS // QUAD
        HALF = QUADS // 2
        leaves = {}
        halves = {}
        es = {}
        others = None
        for t in range(QUADS + 3):
            if t == HALF - 1:
                first = min(share[1][0] for share in SHARES)
                for part in (f_sbuf[:, first:F_SLOTS, :], minus_half_sum[:]):
                    nc.vector.tensor_copy(out=part[:, :, ROWS:WRAPPED], in_=part[:, :, 0:WINDOW])
            if t == HALF:
                f_banks = [turn(q, (1, 0)) for q in range(CHAIN_BANKS)]
            back = t - 3
            if back == HALF:
                add_first_others(others)
            if back >= 0:
                if back % HALF == 0:
                    others = open_others(base_of(back))
                turned = turn_back(back, es[back], others, back % HALF == HALF - 1)
            if t < QUADS:
                chain_ks, pool_ks, scalar_ks = share_of(t)
                by_scalar = work.tile([P, QUAD, len(scalar_ks), WINDOW], F32, name="by_scalar")
                by_pool = work.tile([P, QUAD, len(pool_ks), WINDOW], F32, name="by_pool")
                acc = work.tile([P, QUAD, WINDOW], F32, name="acc")
                leaves[t] = (by_pool, acc, by_scalar)
                for k in scalar_ks:
                    if k == scalar_ks[len(scalar_ks) // 2] and t >= 2:
                        es[t - 2] = exponentials(halves[t - 2])
                    if t == 0:
                        keep_f(k)
                    absolute_differences(t, by_scalar, k)
                if t == 0:
                    for k in (8, 7, 6, 0, 1, 2, 3, 4, 5):
                        keep_f(k)
                    nc.vector.tensor_scalar_mul(
                        out=minus_half_sum[:, 0, 0:ROWS], in0=max_sum[:], scalar1=-0.5
                    )
                for k in pool_ks:
                    pool_maxima(t, by_pool, k)
                for k in chain_ks:
                    chain_link(t, acc, k, f_banks)
                    if k == chain_ks[len(chain_ks) // 2] and back >= 0:
                        sum_over_later(back, turned)
                if t == 0:
                    nc.vector.tensor_copy(out=f_sbuf[:, K, 0:ROWS], in_=in_psum(SHARED_K))
                    nc.vector.scalar_tensor_tensor(
                        out=minus_half_sum[:, 1, 0:ROWS],
                        in0=in_psum(SHARED_K),
                        scalar=-0.5,
                        in1=minus_half_sum[:, 0, 0:ROWS],
                        op0=ALU.mult,
                        op1=ALU.add,
                    )
            else:
                if t - 2 < QUADS:
                    es[t - 2] = exponentials(halves[t - 2])
                sum_over_later(back, turned)
            if 1 <= t <= QUADS:
                halves[t - 1] = add_up(t - 1, *leaves[t - 1])

        nc.scalar.copy(out=late_others[:, 1:], in_=others[:])
        d_t = banks.tile([P, ROW_BLOCKS, J], F32, name="d_t", tag="bank0")
        for b in range(ROW_BLOCKS):
            rows = slice(b * P, (b + 1) * P)
            late = (b + 1) % ROW_BLOCKS * P
            summands = (
                diversity[:, rows],
                late_others[:, late : late + P],
                late_others[:, ROWS + 1 + late : ROWS + 1 + late + P],
                from_later[:, rows],
            )
            for s, summand in enumerate(summands):
                nc.tensor.matmul(
                    out=d_t[:, b, :],
                    lhsT=summand,
                    rhs=identity[:],
                    is_transpose=True,
                    start=(s == 0),
                    stop=(s == len(summands) - 1),
                )
        nc.vector.tensor_copy(out=d_rows[:], in_=d_t[:])
        nc.sync.dma_start(
            out=out[:, IN_F : IN_F + J].rearrange("(b p) j -> p b j", p=P), in_=d_rows[:]
        )
